import numpy as np
import ml_dtypes


def mxq(x, axis, fmt="e4m3"):
    dtype, down = {"e4m3": (ml_dtypes.float8_e4m3fn, 7), "e5m2": (ml_dtypes.float8_e5m2, 14)}[fmt]
    v = np.moveaxis(np.asarray(x, np.float32).astype(ml_dtypes.bfloat16).astype(np.float64), axis, -1)
    blocks = v.reshape(v.shape[:-1] + (-1, 32))
    amax = np.abs(blocks).max(-1, keepdims=True)
    byte = np.maximum(np.where(amax > 0, np.frexp(amax)[1] - 1 + 127, 0) - down, 1)
    scale = np.exp2(byte - 127.0)
    codes = (blocks / scale).astype(np.float32).astype(dtype).astype(np.float64)
    return np.moveaxis((codes * scale).reshape(v.shape), -1, axis)


WIDE = False


def mx_kscale(k):
    if not WIDE:
        return np.ones(k)
    levels = np.array([10, -10, 5, -5, 0])
    a = np.random.permutation(np.resize(levels, k // 512 * 4)).reshape(k // 512, 4)
    idx = np.arange(k)
    return np.exp2(a[idx // 512, idx % 128 // 32])


BF16 = ml_dtypes.bfloat16


def bf(x):
    return np.asarray(x, np.float32).astype(BF16)


def f64(x):
    return np.asarray(x).astype(np.float64)


B, D, ELL = 1024, 1024, 4


def setup_inputs():
    t = mx_kscale(D)
    return {"x": bf(np.random.standard_normal((B, D))),
            "w_j": bf(np.random.standard_normal((D, D)) / np.sqrt(D) * t[:, None]),
            "b_j": bf(np.random.standard_normal(D) * 0.3 * t),
            "w_i": bf(np.random.standard_normal((D, D)) / np.sqrt(D) / t)}


def reference(x, w_j, b_j, w_i):
    x = f64(x)
    th = np.tanh(x)
    phi_j = (mxq(th, 1, "e4m3") @ mxq(f64(w_j), 1, "e4m3").T) + f64(b_j)
    h = (1.0 - th * th) * phi_j
    return mxq(h, 1, "e4m3") @ mxq(f64(w_i), 1, "e4m3").T

@@ -1,0 +1,376 @@
+from contextlib import ExitStack
+
+import concourse.mybir as mybir
+from concourse.masks import make_identity
+
+F32 = mybir.dt.float32
+BF16 = mybir.dt.bfloat16
+U32 = mybir.dt.uint32
+U8 = mybir.dt.uint8
+FP8X4 = mybir.dt.float8_e4m3fn_x4
+ACT = mybir.ActivationFunctionType
+ALU = mybir.AluOpType
+
+P = 128
+B = 1024
+D = 1024
+PACK = 4
+K_PASS = P * PACK
+PASSES = D // K_PASS
+CHUNK = 512
+CHUNKS = B // CHUNK
+ROW_TILES = CHUNK // P
+PLANES = D // P
+WORD_BLOCKS = D // (2 * P)
+
+FLOPS = 2 * 2 * B * D * D
+
+
+def tile_inimnetdisc_pc_kernel(tc, x, w_j, b_j, w_i, out):
+    nc = tc.nc
+    with ExitStack() as ctx:
+        keep = ctx.enter_context(tc.tile_pool(name="keep", bufs=1))
+        wj_stage = ctx.enter_context(tc.tile_pool(name="wj_stage", bufs=3))
+        stage = ctx.enter_context(tc.tile_pool(name="stage", bufs=2))
+        result = ctx.enter_context(tc.tile_pool(name="result", bufs=6))
+        front_psum = ctx.enter_context(tc.psum_pool(name="front_psum", bufs=4))
+        phi_psum = ctx.enter_context(tc.psum_pool(name="phi_psum", bufs=4))
+        ctx.enter_context(tc.manual_schedule())
+
+        x_view = x.rearrange("(c p r) k -> c p r k", c=CHUNKS, p=P)
+        out_view = out.rearrange("(c p r) n -> c p r n", c=CHUNKS, p=P)
+        wj_view = w_j.rearrange("(a p e) k -> a p e k", p=P, e=2)
+        wi_view = w_i.rearrange("(s m p) k -> s p m k", m=ROW_TILES, p=P)
+
+        x_sb = [keep.tile([P, ROW_TILES, D], BF16, name="x_sb%d" % c) for c in range(CHUNKS)]
+        wj_sb = [keep.tile([P, 2, D], BF16, name="wj_sb%d" % a) for a in range(4)]
+        wi_sb = [keep.tile([P, ROW_TILES, D], BF16, name="wi_sb%d" % s) for s in range(2)]
+        t_f32 = [keep.tile([P, PLANES, CHUNK], F32, name="t_f32_%d" % c) for c in range(CHUNKS)]
+        gate = [keep.tile([P, PLANES, CHUNK], F32, name="gate%d" % c) for c in range(CHUNKS)]
+        t_grp = [
+            keep.tile([P, PASSES, CHUNK, PACK], BF16, name="t_grp%d" % c, align_bytes=64)
+            for c in range(CHUNKS)
+        ]
+        t_codes = [keep.tile([P, PASSES * CHUNK], U32, name="t_codes%d" % c, align_bytes=64) for c in range(CHUNKS)]
+        t_scales = [keep.tile([P, PASSES * CHUNK], U8, name="t_scales%d" % c, align_bytes=64) for c in range(CHUNKS)]
+        h_codes = [keep.tile([P, PASSES * CHUNK], U32, name="h_codes%d" % c, align_bytes=64) for c in range(CHUNKS)]
+        h_scales = [keep.tile([P, PASSES * CHUNK], U8, name="h_scales%d" % c, align_bytes=64) for c in range(CHUNKS)]
+        wj_codes = [keep.tile([P, 4 * P], U32, name="wj_codes%d" % a, align_bytes=64) for a in range(4)]
+        wj_scales = [keep.tile([P, 4 * P], U8, name="wj_scales%d" % a, align_bytes=64) for a in range(4)]
+        wi_codes = [keep.tile([P, PASSES * CHUNK], U32, name="wi_codes%d" % s, align_bytes=64) for s in range(2)]
+        wi_scales = [keep.tile([P, PASSES * CHUNK], U8, name="wi_scales%d" % s, align_bytes=64) for s in range(2)]
+
+        def load_x(c, r0, r1):
+            nc.sync.dma_start(out=x_sb[c][:, r0:r1, :], in_=x_view[c, :, r0:r1, :])
+
+        def load_wj(a):
+            nc.sync.dma_start(out=wj_sb[a][:], in_=wj_view[a])
+
+        load_x(0, 0, 1)
+        load_x(0, 1, 2)
+        load_wj(0)
+        load_x(0, 2, 3)
+        load_x(0, 3, 4)
+        load_wj(1)
+        load_wj(2)
+        load_wj(3)
+        load_x(1, 0, 2)
+        load_x(1, 2, 4)
+        for s in range(2):
+            for m0 in range(0, ROW_TILES, 2):
+                nc.sync.dma_start(out=wi_sb[s][:, m0 : m0 + 2, :], in_=wi_view[s, :, m0 : m0 + 2, :])
+
+        ident = keep.tile([P, P], F32, name="ident")
+        make_identity(nc, ident[:])
+
+        bias_bf = keep.tile([P, PLANES], BF16, name="bias_bf")
+        nc.scalar.dma_start(
+            out=bias_bf[:].rearrange("q (a e) -> q a e", e=2),
+            in_=b_j.rearrange("(a q e) -> q a e", q=P, e=2),
+        )
+        bias = keep.tile([P, PLANES], F32, name="bias")
+        nc.vector.tensor_copy(out=bias[:], in_=bias_bf[:])
+
+        banks = {}
+        groups = {}
+
+        def transpose_words(key, rows):
+            bank = front_psum.tile([P, WORD_BLOCKS * P], F32, tag="front")
+            words = rows.bitcast(F32)
+            for v in range(WORD_BLOCKS):
+                nc.tensor.transpose(bank[:, v * P : (v + 1) * P], words[:, v * P : (v + 1) * P], ident[:])
+            banks[key] = bank
+
+        def transpose_x(c, r):
+            transpose_words(("x", c, r), x_sb[c][:, r, :])
+
+        def transpose_wj(a):
+            for e in range(2):
+                transpose_words(("wj", a, e), wj_sb[a][:, e, :])
+
+        def transpose_wi(s):
+            for m in range(ROW_TILES):
+                transpose_words(("wi", s, m), wi_sb[s][:, m, :])
+
+        def copy_out(engine, out_ap, in_ap):
+            if engine is nc.vector:
+                nc.vector.tensor_copy(out=out_ap, in_=in_ap)
+            else:
+                nc.scalar.copy(out=out_ap, in_=in_ap)
+
+        def tanh(c, r):
+            cols = slice(r * P, (r + 1) * P)
+            nc.scalar.activation(
+                out=t_f32[c][:, :, cols].rearrange("q (v e) p -> q v e p", e=2),
+                in_=banks[("x", c, r)][:].bitcast(BF16).rearrange("q (v p e) -> q v e p", v=WORD_BLOCKS, e=2),
+                func=ACT.Tanh,
+            )
+
+        def round_t(c, r):
+            cols = slice(r * P, (r + 1) * P)
+            nc.vector.tensor_copy(
+                out=t_grp[c][:, :, cols, :],
+                in_=t_f32[c][:, :, cols].rearrange("q (g t) j -> q g j t", t=PACK),
+            )
+
+        def quantise_t(c):
+            nc.vector.quantize_mx(
+                out=t_codes[c][:].bitcast(FP8X4),
+                scales=t_scales[c][:],
+                in_=t_grp[c][:].rearrange("q g j t -> q (g j t)"),
+            )
+
+        def copy_wj(engine, a):
+            grp = wj_stage.tile([P, 4 * P * PACK], BF16, tag="wj_grp", align_bytes=64)
+            groups[("wj", a)] = grp
+            grp_words = grp[:].bitcast(F32).rearrange("q (g e p u) -> q g e p u", g=PASSES, e=2, u=2)
+            for e in range(2):
+                copy_out(
+                    engine,
+                    grp_words[:, :, e, :, :],
+                    banks[("wj", a, e)][:].rearrange("q (g u p) -> q g p u", g=PASSES, u=2),
+                )
+
+        def quantise_wj(a):
+            nc.vector.quantize_mx(
+                out=wj_codes[a][:].bitcast(FP8X4), scales=wj_scales[a][:], in_=groups[("wj", a)][:]
+            )
+
+        def copy_wi(s):
+            grp = stage.tile([P, PASSES * CHUNK * PACK], BF16, tag="wi_grp", align_bytes=64)
+            groups[("wi", s)] = grp
+            grp_words = grp[:].bitcast(F32).rearrange("q (g m p u) -> q g m p u", g=PASSES, m=ROW_TILES, u=2)
+            for m in range(ROW_TILES):
+                nc.scalar.copy(
+                    out=grp_words[:, :, m, :, :],
+                    in_=banks[("wi", s, m)][:].rearrange("q (g u p) -> q g p u", g=PASSES, u=2),
+                )
+
+        def quantise_wi(s):
+            nc.vector.quantize_mx(
+                out=wi_codes[s][:].bitcast(FP8X4), scales=wi_scales[s][:], in_=groups[("wi", s)][:]
+            )
+
+        def square(c, g):
+            planes = slice(g * PACK, (g + 1) * PACK)
+            nc.scalar.activation(out=gate[c][:, planes, :], in_=t_f32[c][:, planes, :], func=ACT.Square)
+
+        def one_minus(engine, c, g):
+            planes = slice(g * PACK, (g + 1) * PACK)
+            if engine is nc.vector:
+                nc.vector.tensor_scalar(
+                    out=gate[c][:, planes, :],
+                    in0=gate[c][:, planes, :],
+                    scalar1=-1.0,
+                    scalar2=1.0,
+                    op0=ALU.mult,
+                    op1=ALU.add,
+                )
+            else:
+                nc.scalar.activation(
+                    out=gate[c][:, planes, :], in_=gate[c][:, planes, :], func=ACT.Copy, scale=-1.0, bias=1.0
+                )
+
+        def first_matmul(c, plane):
+            a, e = divmod(plane, 2)
+            acc = phi_psum.tile([P, CHUNK], F32, tag="phi")
+            banks[("phi", c, plane)] = acc
+            for g in range(PASSES):
+                w_cols = slice((g * 2 + e) * P, (g * 2 + e + 1) * P)
+                t_cols = slice(g * CHUNK, (g + 1) * CHUNK)
+                nc.tensor.matmul_mx(
+                    out=acc[:],
+                    lhsT=wj_codes[a][:, w_cols].bitcast(FP8X4),
+                    lhsT_scale=wj_scales[a][:, w_cols],
+                    rhs=t_codes[c][:, t_cols].bitcast(FP8X4),
+                    rhs_scale=t_scales[c][:, t_cols],
+                    start=(g == 0),
+                    stop=(g == PASSES - 1),
+                )
+
+        def new_hidden_planes(c, g):
+            h_pl = stage.tile([P, PACK, CHUNK], BF16, tag="h_pl")
+            groups[("h_pl", c, g)] = h_pl
+
+        def gate_hidden(c, plane, j0, j1):
+            g, t = divmod(plane, PACK)
+            nc.vector.scalar_tensor_tensor(
+                out=groups[("h_pl", c, g)][:, t, j0:j1],
+                in0=banks[("phi", c, plane)][:, j0:j1],
+                scalar=bias[:, plane : plane + 1],
+                in1=gate[c][:, plane, j0:j1],
+                op0=ALU.add,
+                op1=ALU.mult,
+            )
+
+        def regroup_h(c, g, j0, j1):
+            h_grp = stage.tile([P, j1 - j0, PACK], BF16, tag="h_grp", align_bytes=64)
+            groups[("h_grp", c, g, j0)] = h_grp
+            nc.vector.tensor_copy(out=h_grp[:], in_=groups[("h_pl", c, g)][:, :, j0:j1].rearrange("q t j -> q j t"))
+
+        def quantise_h(c, g, j0, j1):
+            h_cols = slice(g * CHUNK + j0, g * CHUNK + j1)
+            nc.vector.quantize_mx(
+                out=h_codes[c][:, h_cols].bitcast(FP8X4),
+                scales=h_scales[c][:, h_cols],
+                in_=groups[("h_grp", c, g, j0)][:].rearrange("q j t -> q (j t)"),
+            )
+
+        def second_matmul(pool, c, r, s, g):
+            if g == 0:
+                if pool is phi_psum:
+                    acc = phi_psum.tile([P, CHUNK], F32, tag="phi")
+                else:
+                    acc = front_psum.tile([P, CHUNK], F32, tag="front")
+                banks[("out", c, r, s)] = acc
+            h_cols = slice(g * CHUNK + r * P, g * CHUNK + (r + 1) * P)
+            w_cols = slice(g * CHUNK, (g + 1) * CHUNK)
+            nc.tensor.matmul_mx(
+                out=banks[("out", c, r, s)][:],
+                lhsT=h_codes[c][:, h_cols].bitcast(FP8X4),
+                lhsT_scale=h_scales[c][:, h_cols],
+                rhs=wi_codes[s][:, w_cols].bitcast(FP8X4),
+                rhs_scale=wi_scales[s][:, w_cols],
+                start=(g == 0),
+                stop=(g == PASSES - 1),
+            )
+
+        def store(engine, c, r, s):
+            res = result.tile([P, CHUNK], F32, tag="res")
+            copy_out(engine, res[:], banks[("out", c, r, s)][:])
+            nc.sync.dma_start(out=out_view[c, :, r, s * CHUNK : (s + 1) * CHUNK], in_=res[:])
+
+        HALF = CHUNK // 2
+        rows = range(ROW_TILES)
+
+        transpose_x(0, 0)
+        tanh(0, 0)
+        transpose_x(0, 1)
+        tanh(0, 1)
+        transpose_wj(0)
+        round_t(0, 0)
+        copy_wj(nc.vector, 0)
+        transpose_x(0, 2)
+        tanh(0, 2)
+        round_t(0, 1)
+        transpose_x(0, 3)
+        tanh(0, 3)
+        transpose_wj(1)
+        round_t(0, 2)
+        quantise_wj(0)
+        transpose_wj(2)
+        square(0, 0)
+        round_t(0, 3)
+        quantise_t(0)
+        copy_wj(nc.scalar, 1)
+        one_minus(nc.vector, 0, 0)
+
+        new_hidden_planes(0, 0)
+        first_matmul(0, 0)
+        first_matmul(0, 1)
+        transpose_wj(3)
+        copy_wj(nc.scalar, 2)
+        gate_hidden(0, 0, 0, CHUNK)
+        gate_hidden(0, 1, 0, CHUNK)
+        quantise_wj(1)
+        first_matmul(0, 2)
+        first_matmul(0, 3)
+        copy_wj(nc.scalar, 3)
+        square(0, 1)
+        gate_hidden(0, 2, 0, CHUNK)
+        gate_hidden(0, 3, 0, CHUNK)
+        for r in rows:
+            transpose_x(1, r)
+            tanh(1, r)
+        quantise_wj(2)
+        quantise_wj(3)
+        regroup_h(0, 0, 0, CHUNK)
+        one_minus(nc.vector, 0, 1)
+        quantise_h(0, 0, 0, CHUNK)
+
+        new_hidden_planes(0, 1)
+        for plane in range(PACK, PLANES):
+            first_matmul(0, plane)
+        transpose_wi(0)
+        square(1, 0)
+        for plane in range(PACK, PLANES):
+            gate_hidden(0, plane, 0, CHUNK)
+        regroup_h(0, 1, 0, CHUNK)
+        copy_wi(0)
+        transpose_wi(1)
+        round_t(1, 0)
+        round_t(1, 1)
+        quantise_h(0, 1, 0, CHUNK)
+        round_t(1, 2)
+        round_t(1, 3)
+        square(1, 1)
+        copy_wi(1)
+        quantise_wi(0)
+        quantise_t(1)
+        one_minus(nc.vector, 1, 0)
+
+        new_hidden_planes(1, 0)
+        for plane in range(PACK):
+            first_matmul(1, plane)
+        one_minus(nc.scalar, 1, 1)
+        for r in rows:
+            for g in range(PASSES):
+                second_matmul(front_psum, 0, r, 0, g)
+        for plane in range(PACK):
+            gate_hidden(1, plane, 0, CHUNK)
+        for r in rows:
+            store(nc.scalar, 0, r, 0)
+        new_hidden_planes(1, 1)
+        for plane in range(PACK, PLANES):
+            first_matmul(1, plane)
+        regroup_h(1, 0, 0, CHUNK)
+        quantise_wi(1)
+        quantise_h(1, 0, 0, CHUNK)
+        for r in rows:
+            for g in range(PASSES):
+                second_matmul(front_psum, 0, r, 1, g)
+        for r in rows:
+            store(nc.scalar, 0, r, 1)
+
+        for plane in range(PACK, PLANES):
+            gate_hidden(1, plane, 0, HALF)
+        regroup_h(1, 1, 0, HALF)
+        quantise_h(1, 1, 0, HALF)
+        for g in range(PASSES):
+            for r in range(0, 2):
+                for s in range(2):
+                    second_matmul(front_psum, 1, r, s, g)
+        for r in range(0, 2):
+            for s in range(2):
+                store(nc.scalar, 1, r, s)
+        for plane in range(PACK, PLANES):
+            gate_hidden(1, plane, HALF, CHUNK)
+        regroup_h(1, 1, HALF, CHUNK)
+        quantise_h(1, 1, HALF, CHUNK)
+        for g in range(PASSES):
+            for r in range(2, ROW_TILES):
+                for s in range(2):
+                    second_matmul(phi_psum, 1, r, s, g)
+        for r in range(2, ROW_TILES):
+            store(nc.vector, 1, r, 0)
+            store(nc.scalar, 1, r, 1)

@@ -35,7 +35,6 @@ def tile_inimnetdisc_pc_kernel(tc, x, w_j, b_j, w_i, out):
         result = ctx.enter_context(tc.tile_pool(name="result", bufs=6))
         front_psum = ctx.enter_context(tc.psum_pool(name="front_psum", bufs=4))
         phi_psum = ctx.enter_context(tc.psum_pool(name="phi_psum", bufs=4))
-        ctx.enter_context(tc.manual_schedule())
 
         x_view = x.rearrange("(c p r) k -> c p r k", c=CHUNKS, p=P)
         out_view = out.rearrange("(c p r) n -> c p r n", c=CHUNKS, p=P)

@@ -17,11 +17,17 @@ D = 1024
 PACK = 4
 K_PASS = P * PACK
 PASSES = D // K_PASS
-CHUNK = 512
+BANK = 512
+CHUNK = BANK
 CHUNKS = B // CHUNK
+HALF = CHUNK // 2
 ROW_TILES = CHUNK // P
 PLANES = D // P
-WORD_BLOCKS = D // (2 * P)
+PAIR = 2
+WORD_BLOCKS = D // (PAIR * P)
+WJ_BLOCKS = D // (PAIR * P)
+WI_HALVES = D // BANK
+RUN = 4
 
 FLOPS = 2 * 2 * B * D * D
 
@@ -38,26 +44,28 @@ def tile_inimnetdisc_pc_kernel(tc, x, w_j, b_j, w_i, out):
 
         x_view = x.rearrange("(c p r) k -> c p r k", c=CHUNKS, p=P)
         out_view = out.rearrange("(c p r) n -> c p r n", c=CHUNKS, p=P)
-        wj_view = w_j.rearrange("(a p e) k -> a p e k", p=P, e=2)
+        wj_view = w_j.rearrange("(a p e) k -> a p e k", p=P, e=PAIR)
         wi_view = w_i.rearrange("(s m p) k -> s p m k", m=ROW_TILES, p=P)
 
         x_sb = [keep.tile([P, ROW_TILES, D], BF16, name="x_sb%d" % c) for c in range(CHUNKS)]
-        wj_sb = [keep.tile([P, 2, D], BF16, name="wj_sb%d" % a) for a in range(4)]
-        wi_sb = [keep.tile([P, ROW_TILES, D], BF16, name="wi_sb%d" % s) for s in range(2)]
+        wj_sb = [keep.tile([P, PAIR, D], BF16, name="wj_sb%d" % a) for a in range(WJ_BLOCKS)]
+        wi_sb = [keep.tile([P, ROW_TILES, D], BF16, name="wi_sb%d" % s) for s in range(WI_HALVES)]
         t_f32 = [keep.tile([P, PLANES, CHUNK], F32, name="t_f32_%d" % c) for c in range(CHUNKS)]
         gate = [keep.tile([P, PLANES, CHUNK], F32, name="gate%d" % c) for c in range(CHUNKS)]
         t_grp = [
             keep.tile([P, PASSES, CHUNK, PACK], BF16, name="t_grp%d" % c, align_bytes=64)
             for c in range(CHUNKS)
         ]
-        t_codes = [keep.tile([P, PASSES * CHUNK], U32, name="t_codes%d" % c, align_bytes=64) for c in range(CHUNKS)]
-        t_scales = [keep.tile([P, PASSES * CHUNK], U8, name="t_scales%d" % c, align_bytes=64) for c in range(CHUNKS)]
-        h_codes = [keep.tile([P, PASSES * CHUNK], U32, name="h_codes%d" % c, align_bytes=64) for c in range(CHUNKS)]
-        h_scales = [keep.tile([P, PASSES * CHUNK], U8, name="h_scales%d" % c, align_bytes=64) for c in range(CHUNKS)]
-        wj_codes = [keep.tile([P, 4 * P], U32, name="wj_codes%d" % a, align_bytes=64) for a in range(4)]
-        wj_scales = [keep.tile([P, 4 * P], U8, name="wj_scales%d" % a, align_bytes=64) for a in range(4)]
-        wi_codes = [keep.tile([P, PASSES * CHUNK], U32, name="wi_codes%d" % s, align_bytes=64) for s in range(2)]
-        wi_scales = [keep.tile([P, PASSES * CHUNK], U8, name="wi_scales%d" % s, align_bytes=64) for s in range(2)]
+
+        def quantised(name, count, words):
+            codes = [keep.tile([P, words], U32, name="%s_codes%d" % (name, i), align_bytes=64) for i in range(count)]
+            scales = [keep.tile([P, words], U8, name="%s_scales%d" % (name, i), align_bytes=64) for i in range(count)]
+            return codes, scales
+
+        t_codes, t_scales = quantised("t", CHUNKS, PASSES * CHUNK)
+        h_codes, h_scales = quantised("h", CHUNKS, PASSES * CHUNK)
+        wj_codes, wj_scales = quantised("wj", WJ_BLOCKS, PASSES * PAIR * P)
+        wi_codes, wi_scales = quantised("wi", WI_HALVES, PASSES * BANK)
 
         def load_x(c, r0, r1):
             nc.sync.dma_start(out=x_sb[c][:, r0:r1, :], in_=x_view[c, :, r0:r1, :])
@@ -70,58 +78,62 @@ def tile_inimnetdisc_pc_kernel(tc, x, w_j, b_j, w_i, out):
         load_wj(0)
         load_x(0, 2, 3)
         load_x(0, 3, 4)
-        load_wj(1)
-        load_wj(2)
-        load_wj(3)
+        for a in range(1, WJ_BLOCKS):
+            load_wj(a)
+        bias_bf16 = keep.tile([P, PLANES], BF16, name="bias_bf16")
+        nc.sync.dma_start(
+            out=bias_bf16[:].rearrange("q (a e) -> q a e", e=PAIR),
+            in_=b_j.rearrange("(a q e) -> q a e", q=P, e=PAIR),
+        )
         load_x(1, 0, 2)
         load_x(1, 2, 4)
-        for s in range(2):
-            for m0 in range(0, ROW_TILES, 2):
-                nc.sync.dma_start(out=wi_sb[s][:, m0 : m0 + 2, :], in_=wi_view[s, :, m0 : m0 + 2, :])
+        for s in range(WI_HALVES):
+            for m in range(0, ROW_TILES, 2):
+                nc.sync.dma_start(out=wi_sb[s][:, m : m + 2, :], in_=wi_view[s, :, m : m + 2, :])
 
         ident = keep.tile([P, P], F32, name="ident")
         make_identity(nc, ident[:])
 
-        bias_bf = keep.tile([P, PLANES], BF16, name="bias_bf")
-        nc.scalar.dma_start(
-            out=bias_bf[:].rearrange("q (a e) -> q a e", e=2),
-            in_=b_j.rearrange("(a q e) -> q a e", q=P, e=2),
-        )
-        bias = keep.tile([P, PLANES], F32, name="bias")
-        nc.vector.tensor_copy(out=bias[:], in_=bias_bf[:])
-
         banks = {}
-        groups = {}
+        staged = {}
 
-        def transpose_words(key, rows):
-            bank = front_psum.tile([P, WORD_BLOCKS * P], F32, tag="front")
+        def front_bank():
+            bank = front_psum.tile([P, BANK], F32, tag="front")
+            return bank
+
+        def phi_bank():
+            bank = phi_psum.tile([P, BANK], F32, tag="phi")
+            return bank
+
+        def vector_copy(out_ap, in_ap):
+            nc.vector.tensor_copy(out=out_ap, in_=in_ap)
+
+        def scalar_copy(out_ap, in_ap):
+            nc.scalar.copy(out=out_ap, in_=in_ap)
+
+        def transpose_words(new_bank, key, rows):
+            banks[key] = new_bank()
             words = rows.bitcast(F32)
             for v in range(WORD_BLOCKS):
-                nc.tensor.transpose(bank[:, v * P : (v + 1) * P], words[:, v * P : (v + 1) * P], ident[:])
-            banks[key] = bank
+                block = slice(v * P, (v + 1) * P)
+                nc.tensor.transpose(banks[key][:, block], words[:, block], ident[:])
 
         def transpose_x(c, r):
-            transpose_words(("x", c, r), x_sb[c][:, r, :])
+            transpose_words(front_bank, ("x", c, r), x_sb[c][:, r, :])
 
-        def transpose_wj(a):
-            for e in range(2):
-                transpose_words(("wj", a, e), wj_sb[a][:, e, :])
+        def transpose_wj(new_bank, a):
+            for e in range(PAIR):
+                transpose_words(new_bank, ("wj", a, e), wj_sb[a][:, e, :])
 
         def transpose_wi(s):
             for m in range(ROW_TILES):
-                transpose_words(("wi", s, m), wi_sb[s][:, m, :])
-
-        def copy_out(engine, out_ap, in_ap):
-            if engine is nc.vector:
-                nc.vector.tensor_copy(out=out_ap, in_=in_ap)
-            else:
-                nc.scalar.copy(out=out_ap, in_=in_ap)
+                transpose_words(front_bank, ("wi", s, m), wi_sb[s][:, m, :])
 
         def tanh(c, r):
             cols = slice(r * P, (r + 1) * P)
             nc.scalar.activation(
-                out=t_f32[c][:, :, cols].rearrange("q (v e) p -> q v e p", e=2),
-                in_=banks[("x", c, r)][:].bitcast(BF16).rearrange("q (v p e) -> q v e p", v=WORD_BLOCKS, e=2),
+                out=t_f32[c][:, :, cols].rearrange("q (v e) p -> q v e p", e=PAIR),
+                in_=banks[("x", c, r)][:].bitcast(BF16).rearrange("q (v p e) -> q v e p", v=WORD_BLOCKS, e=PAIR),
                 func=ACT.Tanh,
             )
 
@@ -139,66 +151,62 @@ def tile_inimnetdisc_pc_kernel(tc, x, w_j, b_j, w_i, out):
                 in_=t_grp[c][:].rearrange("q g j t -> q (g j t)"),
             )
 
-        def copy_wj(engine, a):
-            grp = wj_stage.tile([P, 4 * P * PACK], BF16, tag="wj_grp", align_bytes=64)
-            groups[("wj", a)] = grp
-            grp_words = grp[:].bitcast(F32).rearrange("q (g e p u) -> q g e p u", g=PASSES, e=2, u=2)
-            for e in range(2):
-                copy_out(
-                    engine,
-                    grp_words[:, :, e, :, :],
-                    banks[("wj", a, e)][:].rearrange("q (g u p) -> q g p u", g=PASSES, u=2),
-                )
+        def words_by_pass(bank):
+            return bank[:].rearrange("q (g u p) -> q g p u", g=PASSES, u=PAIR)
+
+        def copy_wj(copy, a):
+            wj_grp = wj_stage.tile([P, PASSES * PAIR * P * PACK], BF16, tag="wj_grp", align_bytes=64)
+            staged[("wj", a)] = wj_grp
+            grp_words = wj_grp[:].bitcast(F32).rearrange("q (g e p u) -> q g e p u", g=PASSES, e=PAIR, u=PAIR)
+            for e in range(PAIR):
+                copy(grp_words[:, :, e, :, :], words_by_pass(banks[("wj", a, e)]))
 
         def quantise_wj(a):
             nc.vector.quantize_mx(
-                out=wj_codes[a][:].bitcast(FP8X4), scales=wj_scales[a][:], in_=groups[("wj", a)][:]
+                out=wj_codes[a][:].bitcast(FP8X4), scales=wj_scales[a][:], in_=staged[("wj", a)][:]
             )
 
-        def copy_wi(s):
-            grp = stage.tile([P, PASSES * CHUNK * PACK], BF16, tag="wi_grp", align_bytes=64)
-            groups[("wi", s)] = grp
-            grp_words = grp[:].bitcast(F32).rearrange("q (g m p u) -> q g m p u", g=PASSES, m=ROW_TILES, u=2)
+        def copy_wi(copy, s):
+            wi_grp = stage.tile([P, PASSES * BANK * PACK], BF16, tag="wi_grp", align_bytes=64)
+            staged[("wi", s)] = wi_grp
+            grp_words = wi_grp[:].bitcast(F32).rearrange("q (g m p u) -> q g m p u", g=PASSES, m=ROW_TILES, u=PAIR)
             for m in range(ROW_TILES):
-                nc.scalar.copy(
-                    out=grp_words[:, :, m, :, :],
-                    in_=banks[("wi", s, m)][:].rearrange("q (g u p) -> q g p u", g=PASSES, u=2),
-                )
+                copy(grp_words[:, :, m, :, :], words_by_pass(banks[("wi", s, m)]))
 
         def quantise_wi(s):
             nc.vector.quantize_mx(
-                out=wi_codes[s][:].bitcast(FP8X4), scales=wi_scales[s][:], in_=groups[("wi", s)][:]
+                out=wi_codes[s][:].bitcast(FP8X4), scales=wi_scales[s][:], in_=staged[("wi", s)][:]
             )
 
-        def square(c, g):
-            planes = slice(g * PACK, (g + 1) * PACK)
-            nc.scalar.activation(out=gate[c][:, planes, :], in_=t_f32[c][:, planes, :], func=ACT.Square)
+        def planes_of(g):
+            return slice(g * PACK, (g + 1) * PACK)
 
-        def one_minus(engine, c, g):
-            planes = slice(g * PACK, (g + 1) * PACK)
-            if engine is nc.vector:
-                nc.vector.tensor_scalar(
-                    out=gate[c][:, planes, :],
-                    in0=gate[c][:, planes, :],
-                    scalar1=-1.0,
-                    scalar2=1.0,
-                    op0=ALU.mult,
-                    op1=ALU.add,
-                )
-            else:
-                nc.scalar.activation(
-                    out=gate[c][:, planes, :], in_=gate[c][:, planes, :], func=ACT.Copy, scale=-1.0, bias=1.0
-                )
+        def square(c, g):
+            nc.scalar.activation(out=gate[c][:, planes_of(g), :], in_=t_f32[c][:, planes_of(g), :], func=ACT.Square)
+
+        def one_minus_on_vector(c, g):
+            nc.vector.tensor_scalar(
+                out=gate[c][:, planes_of(g), :],
+                in0=gate[c][:, planes_of(g), :],
+                scalar1=-1.0,
+                scalar2=1.0,
+                op0=ALU.mult,
+                op1=ALU.add,
+            )
+
+        def one_minus_on_scalar(c, g):
+            nc.scalar.activation(
+                out=gate[c][:, planes_of(g), :], in_=gate[c][:, planes_of(g), :], func=ACT.Copy, scale=-1.0, bias=1.0
+            )
 
         def first_matmul(c, plane):
-            a, e = divmod(plane, 2)
-            acc = phi_psum.tile([P, CHUNK], F32, tag="phi")
-            banks[("phi", c, plane)] = acc
+            a, e = divmod(plane, PAIR)
+            banks[("phi", c, plane)] = phi_bank()
             for g in range(PASSES):
-                w_cols = slice((g * 2 + e) * P, (g * 2 + e + 1) * P)
+                w_cols = slice((g * PAIR + e) * P, (g * PAIR + e + 1) * P)
                 t_cols = slice(g * CHUNK, (g + 1) * CHUNK)
                 nc.tensor.matmul_mx(
-                    out=acc[:],
+                    out=banks[("phi", c, plane)][:],
                     lhsT=wj_codes[a][:, w_cols].bitcast(FP8X4),
                     lhsT_scale=wj_scales[a][:, w_cols],
                     rhs=t_codes[c][:, t_cols].bitcast(FP8X4),
@@ -207,16 +215,16 @@ def tile_inimnetdisc_pc_kernel(tc, x, w_j, b_j, w_i, out):
                     stop=(g == PASSES - 1),
                 )
 
-        def new_hidden_planes(c, g):
-            h_pl = stage.tile([P, PACK, CHUNK], BF16, tag="h_pl")
-            groups[("h_pl", c, g)] = h_pl
+        def new_h_planes(c, g):
+            h_planes = stage.tile([P, PACK, CHUNK], BF16, tag="h_planes")
+            staged[("h_planes", c, g)] = h_planes
 
-        def gate_hidden(c, plane, j0, j1):
+        def gate_phi(c, plane, j0, j1):
             g, t = divmod(plane, PACK)
             nc.vector.scalar_tensor_tensor(
-                out=groups[("h_pl", c, g)][:, t, j0:j1],
+                out=staged[("h_planes", c, g)][:, t, j0:j1],
                 in0=banks[("phi", c, plane)][:, j0:j1],
-                scalar=bias[:, plane : plane + 1],
+                scalar=bias_bf16[:, plane : plane + 1],
                 in1=gate[c][:, plane, j0:j1],
                 op0=ALU.add,
                 op1=ALU.mult,
@@ -224,26 +232,25 @@ def tile_inimnetdisc_pc_kernel(tc, x, w_j, b_j, w_i, out):
 
         def regroup_h(c, g, j0, j1):
             h_grp = stage.tile([P, j1 - j0, PACK], BF16, tag="h_grp", align_bytes=64)
-            groups[("h_grp", c, g, j0)] = h_grp
-            nc.vector.tensor_copy(out=h_grp[:], in_=groups[("h_pl", c, g)][:, :, j0:j1].rearrange("q t j -> q j t"))
+            staged[("h_grp", c, g, j0)] = h_grp
+            nc.vector.tensor_copy(
+                out=h_grp[:].rearrange("q (n i) t -> q n t i", i=RUN),
+                in_=staged[("h_planes", c, g)][:, :, j0:j1].rearrange("q t (n i) -> q n t i", i=RUN),
+            )
 
         def quantise_h(c, g, j0, j1):
             h_cols = slice(g * CHUNK + j0, g * CHUNK + j1)
             nc.vector.quantize_mx(
                 out=h_codes[c][:, h_cols].bitcast(FP8X4),
                 scales=h_scales[c][:, h_cols],
-                in_=groups[("h_grp", c, g, j0)][:].rearrange("q j t -> q (j t)"),
+                in_=staged[("h_grp", c, g, j0)][:].rearrange("q j t -> q (j t)"),
             )
 
-        def second_matmul(pool, c, r, s, g):
+        def second_matmul(new_bank, c, r, s, g):
             if g == 0:
-                if pool is phi_psum:
-                    acc = phi_psum.tile([P, CHUNK], F32, tag="phi")
-                else:
-                    acc = front_psum.tile([P, CHUNK], F32, tag="front")
-                banks[("out", c, r, s)] = acc
+                banks[("out", c, r, s)] = new_bank()
             h_cols = slice(g * CHUNK + r * P, g * CHUNK + (r + 1) * P)
-            w_cols = slice(g * CHUNK, (g + 1) * CHUNK)
+            w_cols = slice(g * BANK, (g + 1) * BANK)
             nc.tensor.matmul_mx(
                 out=banks[("out", c, r, s)][:],
                 lhsT=h_codes[c][:, h_cols].bitcast(FP8X4),
@@ -254,68 +261,69 @@ def tile_inimnetdisc_pc_kernel(tc, x, w_j, b_j, w_i, out):
                 stop=(g == PASSES - 1),
             )
 
-        def store(engine, c, r, s):
-            res = result.tile([P, CHUNK], F32, tag="res")
-            copy_out(engine, res[:], banks[("out", c, r, s)][:])
-            nc.sync.dma_start(out=out_view[c, :, r, s * CHUNK : (s + 1) * CHUNK], in_=res[:])
+        def store(copy, c, r, s):
+            res = result.tile([P, BANK], F32, tag="res")
+            copy(res[:], banks[("out", c, r, s)][:])
+            nc.sync.dma_start(out=out_view[c, :, r, s * BANK : (s + 1) * BANK], in_=res[:])
 
-        HALF = CHUNK // 2
         rows = range(ROW_TILES)
+        first_planes = range(PACK)
+        last_planes = range(PACK, PLANES)
 
         transpose_x(0, 0)
         tanh(0, 0)
         transpose_x(0, 1)
         tanh(0, 1)
-        transpose_wj(0)
+        transpose_wj(phi_bank, 0)
         round_t(0, 0)
-        copy_wj(nc.vector, 0)
+        copy_wj(vector_copy, 0)
         transpose_x(0, 2)
         tanh(0, 2)
         round_t(0, 1)
         transpose_x(0, 3)
         tanh(0, 3)
-        transpose_wj(1)
+        transpose_wj(phi_bank, 1)
         round_t(0, 2)
         quantise_wj(0)
-        transpose_wj(2)
+        transpose_wj(front_bank, 2)
         square(0, 0)
         round_t(0, 3)
         quantise_t(0)
-        copy_wj(nc.scalar, 1)
-        one_minus(nc.vector, 0, 0)
+        copy_wj(scalar_copy, 1)
+        one_minus_on_vector(0, 0)
 
-        new_hidden_planes(0, 0)
+        new_h_planes(0, 0)
         first_matmul(0, 0)
         first_matmul(0, 1)
-        transpose_wj(3)
-        copy_wj(nc.scalar, 2)
-        gate_hidden(0, 0, 0, CHUNK)
-        gate_hidden(0, 1, 0, CHUNK)
+        transpose_wj(front_bank, 3)
+        copy_wj(scalar_copy, 2)
+        gate_phi(0, 0, 0, CHUNK)
+        gate_phi(0, 1, 0, CHUNK)
         quantise_wj(1)
         first_matmul(0, 2)
         first_matmul(0, 3)
-        copy_wj(nc.scalar, 3)
+        copy_wj(scalar_copy, 3)
         square(0, 1)
-        gate_hidden(0, 2, 0, CHUNK)
-        gate_hidden(0, 3, 0, CHUNK)
+        gate_phi(0, 2, 0, CHUNK)
+        gate_phi(0, 3, 0, CHUNK)
         for r in rows:
             transpose_x(1, r)
             tanh(1, r)
         quantise_wj(2)
         quantise_wj(3)
         regroup_h(0, 0, 0, CHUNK)
-        one_minus(nc.vector, 0, 1)
+        one_minus_on_vector(0, 1)
         quantise_h(0, 0, 0, CHUNK)
 
-        new_hidden_planes(0, 1)
-        for plane in range(PACK, PLANES):
+        new_h_planes(0, 1)
+        for plane in last_planes:
             first_matmul(0, plane)
         transpose_wi(0)
         square(1, 0)
-        for plane in range(PACK, PLANES):
-            gate_hidden(0, plane, 0, CHUNK)
+        for plane in last_planes:
+            gate_phi(0, plane, 0, CHUNK)
         regroup_h(0, 1, 0, CHUNK)
-        copy_wi(0)
+        copy_wi(scalar_copy, 0)
         transpose_wi(1)
         round_t(1, 0)
         round_t(1, 1)
@@ -323,53 +331,43 @@ def tile_inimnetdisc_pc_kernel(tc, x, w_j, b_j, w_i, out):
         round_t(1, 2)
         round_t(1, 3)
         square(1, 1)
-        copy_wi(1)
+        copy_wi(scalar_copy, 1)
         quantise_wi(0)
         quantise_t(1)
-        one_minus(nc.vector, 1, 0)
+        one_minus_on_vector(1, 0)
 
-        new_hidden_planes(1, 0)
-        for plane in range(PACK):
+        new_h_planes(1, 0)
+        for plane in first_planes:
             first_matmul(1, plane)
-        one_minus(nc.scalar, 1, 1)
+        one_minus_on_scalar(1, 1)
         for r in rows:
             for g in range(PASSES):
-                second_matmul(front_psum, 0, r, 0, g)
-        for plane in range(PACK):
-            gate_hidden(1, plane, 0, CHUNK)
+                second_matmul(front_bank, 0, r, 0, g)
+        for plane in first_planes:
+            gate_phi(1, plane, 0, CHUNK)
         for r in rows:
-            store(nc.scalar, 0, r, 0)
-        new_hidden_planes(1, 1)
-        for plane in range(PACK, PLANES):
+            store(scalar_copy, 0, r, 0)
+        new_h_planes(1, 1)
+        for plane in last_planes:
             first_matmul(1, plane)
         regroup_h(1, 0, 0, CHUNK)
         quantise_wi(1)
         quantise_h(1, 0, 0, CHUNK)
         for r in rows:
             for g in range(PASSES):
-                second_matmul(front_psum, 0, r, 1, g)
+                second_matmul(front_bank, 0, r, 1, g)
         for r in rows:
-            store(nc.scalar, 0, r, 1)
+            store(scalar_copy, 0, r, 1)
 
-        for plane in range(PACK, PLANES):
-            gate_hidden(1, plane, 0, HALF)
-        regroup_h(1, 1, 0, HALF)
-        quantise_h(1, 1, 0, HALF)
-        for g in range(PASSES):
-            for r in range(0, 2):
-                for s in range(2):
-                    second_matmul(front_psum, 1, r, s, g)
-        for r in range(0, 2):
-            for s in range(2):
-                store(nc.scalar, 1, r, s)
-        for plane in range(PACK, PLANES):
-            gate_hidden(1, plane, HALF, CHUNK)
-        regroup_h(1, 1, HALF, CHUNK)
-        quantise_h(1, 1, HALF, CHUNK)
-        for g in range(PASSES):
-            for r in range(2, ROW_TILES):
-                for s in range(2):
-                    second_matmul(phi_psum, 1, r, s, g)
-        for r in range(2, ROW_TILES):
-            store(nc.vector, 1, r, 0)
-            store(nc.scalar, 1, r, 1)
+        for j0, half_rows, new_bank in ((0, (0, 1), front_bank), (HALF, (2, 3), phi_bank)):
+            for plane in last_planes:
+                gate_phi(1, plane, j0, j0 + HALF)
+            regroup_h(1, 1, j0, j0 + HALF)
+            quantise_h(1, 1, j0, j0 + HALF)
+            for g in range(PASSES):
+                for r in half_rows:
+                    for s in range(WI_HALVES):
+                        second_matmul(new_bank, 1, r, s, g)
+            for r in half_rows:
+                store(scalar_copy if j0 == 0 else vector_copy, 1, r, 0)
+                store(scalar_copy, 1, r, 1)

@@ -18,17 +18,16 @@ PACK = 4
 K_PASS = P * PACK
 PASSES = D // K_PASS
 BANK = 512
-CHUNK = BANK
-CHUNKS = B // CHUNK
-HALF = CHUNK // 2
-ROW_TILES = CHUNK // P
 PLANES = D // P
 PAIR = 2
 WORD_BLOCKS = D // (PAIR * P)
 WJ_BLOCKS = D // (PAIR * P)
 WI_HALVES = D // BANK
+ROW_TILES = BANK // P
 RUN = 4
-
+WIDTHS = (512, 512)
+STARTS = [sum(WIDTHS[:c]) for c in range(len(WIDTHS))]
+CHUNKS = len(WIDTHS)
 FLOPS = 2 * 2 * B * D * D
 
 
@@ -36,80 +35,79 @@ def tile_inimnetdisc_pc_kernel(tc, x, w_j, b_j, w_i, out):
     nc = tc.nc
     with ExitStack() as ctx:
         keep = ctx.enter_context(tc.tile_pool(name="keep", bufs=1))
-        wj_stage = ctx.enter_context(tc.tile_pool(name="wj_stage", bufs=3))
+        wj_stage = ctx.enter_context(tc.tile_pool(name="wj_stage", bufs=4))
         stage = ctx.enter_context(tc.tile_pool(name="stage", bufs=2))
         result = ctx.enter_context(tc.tile_pool(name="result", bufs=6))
         front_psum = ctx.enter_context(tc.psum_pool(name="front_psum", bufs=4))
         phi_psum = ctx.enter_context(tc.psum_pool(name="phi_psum", bufs=4))
 
-        x_view = x.rearrange("(c p r) k -> c p r k", c=CHUNKS, p=P)
-        out_view = out.rearrange("(c p r) n -> c p r n", c=CHUNKS, p=P)
+        def rows_view(dram, c):
+            part = dram[STARTS[c] : STARTS[c] + WIDTHS[c], :]
+            return part.rearrange("(p r) k -> p r k", p=P)
+
+        x_view = [rows_view(x, c) for c in range(CHUNKS)]
+        out_view = [rows_view(out, c) for c in range(CHUNKS)]
         wj_view = w_j.rearrange("(a p e) k -> a p e k", p=P, e=PAIR)
         wi_view = w_i.rearrange("(s m p) k -> s p m k", m=ROW_TILES, p=P)
 
-        x_sb = [keep.tile([P, ROW_TILES, D], BF16, name="x_sb%d" % c) for c in range(CHUNKS)]
+        x_sb = [keep.tile([P, WIDTHS[c] // P, D], BF16, name="x_sb%d" % c) for c in range(CHUNKS)]
         wj_sb = [keep.tile([P, PAIR, D], BF16, name="wj_sb%d" % a) for a in range(WJ_BLOCKS)]
         wi_sb = [keep.tile([P, ROW_TILES, D], BF16, name="wi_sb%d" % s) for s in range(WI_HALVES)]
-        t_f32 = [keep.tile([P, PLANES, CHUNK], F32, name="t_f32_%d" % c) for c in range(CHUNKS)]
-        gate = [keep.tile([P, PLANES, CHUNK], F32, name="gate%d" % c) for c in range(CHUNKS)]
-        t_grp = [
-            keep.tile([P, PASSES, CHUNK, PACK], BF16, name="t_grp%d" % c, align_bytes=64)
-            for c in range(CHUNKS)
-        ]
+        t_f32 = [keep.tile([P, PLANES, WIDTHS[c]], F32, name="t_f32_%d" % c) for c in range(CHUNKS)]
+        gate = [keep.tile([P, PLANES, WIDTHS[c]], F32, name="gate%d" % c) for c in range(CHUNKS)]
+        t_grp = [keep.tile([P, PASSES, WIDTHS[c], PACK], BF16, name="t_grp%d" % c, align_bytes=64) for c in range(CHUNKS)]
 
-        def quantised(name, count, words):
-            codes = [keep.tile([P, words], U32, name="%s_codes%d" % (name, i), align_bytes=64) for i in range(count)]
-            scales = [keep.tile([P, words], U8, name="%s_scales%d" % (name, i), align_bytes=64) for i in range(count)]
+        def quantised(name, words_of):
+            codes = [keep.tile([P, w], U32, name="%s_codes%d" % (name, i), align_bytes=64) for i, w in enumerate(words_of)]
+            scales = [keep.tile([P, w], U8, name="%s_scales%d" % (name, i), align_bytes=64) for i, w in enumerate(words_of)]
             return codes, scales
 
-        t_codes, t_scales = quantised("t", CHUNKS, PASSES * CHUNK)
-        h_codes, h_scales = quantised("h", CHUNKS, PASSES * CHUNK)
-        wj_codes, wj_scales = quantised("wj", WJ_BLOCKS, PASSES * PAIR * P)
-        wi_codes, wi_scales = quantised("wi", WI_HALVES, PASSES * BANK)
-
-        def load_x(c, r0, r1):
-            nc.sync.dma_start(out=x_sb[c][:, r0:r1, :], in_=x_view[c, :, r0:r1, :])
-
-        def load_wj(a):
-            nc.sync.dma_start(out=wj_sb[a][:], in_=wj_view[a])
-
-        load_x(0, 0, 1)
-        load_x(0, 1, 2)
-        load_wj(0)
-        load_x(0, 2, 3)
-        load_x(0, 3, 4)
-        for a in range(1, WJ_BLOCKS):
-            load_wj(a)
-        bias_bf16 = keep.tile([P, PLANES], BF16, name="bias_bf16")
-        nc.sync.dma_start(
-            out=bias_bf16[:].rearrange("q (a e) -> q a e", e=PAIR),
-            in_=b_j.rearrange("(a q e) -> q a e", q=P, e=PAIR),
-        )
-        load_x(1, 0, 2)
-        load_x(1, 2, 4)
-        for s in range(WI_HALVES):
-            for m in range(0, ROW_TILES, 2):
-                nc.sync.dma_start(out=wi_sb[s][:, m : m + 2, :], in_=wi_view[s, :, m : m + 2, :])
+        t_codes, t_scales = quantised("t", [PASSES * w for w in WIDTHS])
+        h_codes, h_scales = quantised("h", [PASSES * w for w in WIDTHS])
+        wj_codes, wj_scales = quantised("wj", [PASSES * PAIR * P] * WJ_BLOCKS)
+        wi_codes, wi_scales = quantised("wi", [PASSES * BANK] * WI_HALVES)
 
         ident = keep.tile([P, P], F32, name="ident")
         make_identity(nc, ident[:])
+        bias_bf16 = keep.tile([P, PLANES], BF16, name="bias_bf16")
 
         banks = {}
         staged = {}
+        zeros = keep.tile([P, BANK], BF16, name="zeros")
 
-        def front_bank():
+        def warm(n, new_bank):
+            bank = new_bank()
+            for i in range(n):
+                nc.tensor.matmul(bank[:], lhsT=zeros[:, :P], rhs=zeros[:], start=True, stop=True)
+
+        def front():
             bank = front_psum.tile([P, BANK], F32, tag="front")
             return bank
 
-        def phi_bank():
+        def phi():
             bank = phi_psum.tile([P, BANK], F32, tag="phi")
             return bank
 
-        def vector_copy(out_ap, in_ap):
+        def vec(out_ap, in_ap):
             nc.vector.tensor_copy(out=out_ap, in_=in_ap)
 
-        def scalar_copy(out_ap, in_ap):
+        def sca(out_ap, in_ap):
             nc.scalar.copy(out=out_ap, in_=in_ap)
+
+        def load_x(c, r0, r1):
+            nc.sync.dma_start(out=x_sb[c][:, r0:r1, :], in_=x_view[c][:, r0:r1, :])
+
+        def load_wj(a, e0=0, e1=PAIR):
+            nc.sync.dma_start(out=wj_sb[a][:, e0:e1, :], in_=wj_view[a][:, e0:e1, :])
+
+        def load_wi(s, m0, m1):
+            nc.sync.dma_start(out=wi_sb[s][:, m0:m1, :], in_=wi_view[s][:, m0:m1, :])
+
+        def load_bias():
+            nc.sync.dma_start(
+                out=bias_bf16[:].rearrange("q (a e) -> q a e", e=PAIR),
+                in_=b_j.rearrange("(a q e) -> q a e", q=P, e=PAIR),
+            )
 
         def transpose_words(new_bank, key, rows):
             banks[key] = new_bank()
@@ -118,16 +116,14 @@ def tile_inimnetdisc_pc_kernel(tc, x, w_j, b_j, w_i, out):
                 block = slice(v * P, (v + 1) * P)
                 nc.tensor.transpose(banks[key][:, block], words[:, block], ident[:])
 
-        def transpose_x(c, r):
-            transpose_words(front_bank, ("x", c, r), x_sb[c][:, r, :])
+        def tx(c, r, new_bank=front):
+            transpose_words(new_bank, ("x", c, r), x_sb[c][:, r, :])
 
-        def transpose_wj(new_bank, a):
-            for e in range(PAIR):
-                transpose_words(new_bank, ("wj", a, e), wj_sb[a][:, e, :])
+        def twj(a, e, new_bank=front):
+            transpose_words(new_bank, ("wj", a, e), wj_sb[a][:, e, :])
 
-        def transpose_wi(s):
-            for m in range(ROW_TILES):
-                transpose_words(front_bank, ("wi", s, m), wi_sb[s][:, m, :])
+        def twi(s, m, new_bank=front):
+            transpose_words(new_bank, ("wi", s, m), wi_sb[s][:, m, :])
 
         def tanh(c, r):
             cols = slice(r * P, (r + 1) * P)
@@ -137,14 +133,14 @@ def tile_inimnetdisc_pc_kernel(tc, x, w_j, b_j, w_i, out):
                 func=ACT.Tanh,
             )
 
-        def round_t(c, r):
+        def rnd(c, r):
             cols = slice(r * P, (r + 1) * P)
             nc.vector.tensor_copy(
                 out=t_grp[c][:, :, cols, :],
                 in_=t_f32[c][:, :, cols].rearrange("q (g t) j -> q g j t", t=PACK),
             )
 
-        def quantise_t(c):
+        def qt(c):
             nc.vector.quantize_mx(
                 out=t_codes[c][:].bitcast(FP8X4),
                 scales=t_scales[c][:],
@@ -154,28 +150,30 @@ def tile_inimnetdisc_pc_kernel(tc, x, w_j, b_j, w_i, out):
         def words_by_pass(bank):
             return bank[:].rearrange("q (g u p) -> q g p u", g=PASSES, u=PAIR)
 
-        def copy_wj(copy, a):
-            wj_grp = wj_stage.tile([P, PASSES * PAIR * P * PACK], BF16, tag="wj_grp", align_bytes=64)
-            staged[("wj", a)] = wj_grp
-            grp_words = wj_grp[:].bitcast(F32).rearrange("q (g e p u) -> q g e p u", g=PASSES, e=PAIR, u=PAIR)
-            for e in range(PAIR):
-                copy(grp_words[:, :, e, :, :], words_by_pass(banks[("wj", a, e)]))
+        def cwj(a, e, copy):
+            if e == 0:
+                wj_grp = wj_stage.tile([P, PASSES * PAIR * P * PACK], BF16, tag="wj_grp", align_bytes=64)
+                staged[("wj", a)] = wj_grp
+            grp_words = staged[("wj", a)][:].bitcast(F32).rearrange("q (g e p u) -> q g e p u", g=PASSES, e=PAIR, u=PAIR)
+            copy(grp_words[:, :, e, :, :], words_by_pass(banks[("wj", a, e)]))
 
-        def quantise_wj(a):
+        def qwj(a):
             nc.vector.quantize_mx(
                 out=wj_codes[a][:].bitcast(FP8X4), scales=wj_scales[a][:], in_=staged[("wj", a)][:]
             )
 
-        def copy_wi(copy, s):
-            wi_grp = stage.tile([P, PASSES * BANK * PACK], BF16, tag="wi_grp", align_bytes=64)
-            staged[("wi", s)] = wi_grp
-            grp_words = wi_grp[:].bitcast(F32).rearrange("q (g m p u) -> q g m p u", g=PASSES, m=ROW_TILES, u=PAIR)
-            for m in range(ROW_TILES):
-                copy(grp_words[:, :, m, :, :], words_by_pass(banks[("wi", s, m)]))
+        def cwi(s, m, copy):
+            if m == 0:
+                wi_grp = stage.tile([P, PASSES * BANK * PACK], BF16, tag="wi_grp", align_bytes=64)
+                staged[("wi", s)] = wi_grp
+            grp_words = staged[("wi", s)][:].bitcast(F32).rearrange("q (g m p u) -> q g m p u", g=PASSES, m=ROW_TILES, u=PAIR)
+            copy(grp_words[:, :, m, :, :], words_by_pass(banks[("wi", s, m)]))
 
-        def quantise_wi(s):
+        def qwi(s, g0=0, g1=PASSES):
+            words = slice(g0 * BANK, g1 * BANK)
             nc.vector.quantize_mx(
-                out=wi_codes[s][:].bitcast(FP8X4), scales=wi_scales[s][:], in_=staged[("wi", s)][:]
+                out=wi_codes[s][:, words].bitcast(FP8X4), scales=wi_scales[s][:, words],
+                in_=staged[("wi", s)][:, g0 * BANK * PACK : g1 * BANK * PACK],
             )
 
         def planes_of(g):
@@ -184,29 +182,38 @@ def tile_inimnetdisc_pc_kernel(tc, x, w_j, b_j, w_i, out):
         def square(c, g):
             nc.scalar.activation(out=gate[c][:, planes_of(g), :], in_=t_f32[c][:, planes_of(g), :], func=ACT.Square)
 
-        def one_minus_on_vector(c, g):
-            nc.vector.tensor_scalar(
-                out=gate[c][:, planes_of(g), :],
-                in0=gate[c][:, planes_of(g), :],
-                scalar1=-1.0,
-                scalar2=1.0,
-                op0=ALU.mult,
-                op1=ALU.add,
-            )
+        def om(c, g, eng):
+            dst = gate[c][:, planes_of(g), :]
+            if eng == "v":
+                nc.vector.tensor_scalar(out=dst, in0=dst, scalar1=-1.0, scalar2=1.0, op0=ALU.mult, op1=ALU.add)
+            elif eng == "g":
+                nc.gpsimd.tensor_scalar(out=dst, in0=dst, scalar1=-1.0, scalar2=1.0, op0=ALU.mult, op1=ALU.add)
+            else:
+                nc.scalar.activation(out=dst, in_=dst, func=ACT.Copy, scale=-1.0, bias=1.0)
 
-        def one_minus_on_scalar(c, g):
-            nc.scalar.activation(
-                out=gate[c][:, planes_of(g), :], in_=gate[c][:, planes_of(g), :], func=ACT.Copy, scale=-1.0, bias=1.0
-            )
+        def less(c, g, eng):
+            dst = gate[c][:, planes_of(g), :]
+            src = t_f32[c][:, planes_of(g), :]
+            if eng == "v":
+                nc.vector.tensor_scalar(out=dst, in0=src, scalar1=-1.0, scalar2=1.0, op0=ALU.mult, op1=ALU.add)
+            elif eng == "g":
+                nc.gpsimd.tensor_scalar(out=dst, in0=src, scalar1=-1.0, scalar2=1.0, op0=ALU.mult, op1=ALU.add)
+            else:
+                nc.scalar.activation(out=dst, in_=src, func=ACT.Copy, scale=-1.0, bias=1.0)
 
-        def first_matmul(c, plane):
+        def mm1(c, plane, new_bank=phi, pair=False):
             a, e = divmod(plane, PAIR)
-            banks[("phi", c, plane)] = phi_bank()
+            w = WIDTHS[c]
+            if not pair or e == 0:
+                banks[("phi", c, plane)] = new_bank()
+            else:
+                banks[("phi", c, plane)] = banks[("phi", c, plane - 1)]
+            o0 = w if (pair and e == 1) else 0
             for g in range(PASSES):
                 w_cols = slice((g * PAIR + e) * P, (g * PAIR + e + 1) * P)
-                t_cols = slice(g * CHUNK, (g + 1) * CHUNK)
+                t_cols = slice(g * w, (g + 1) * w)
                 nc.tensor.matmul_mx(
-                    out=banks[("phi", c, plane)][:],
+                    out=banks[("phi", c, plane)][:, o0 : o0 + w],
                     lhsT=wj_codes[a][:, w_cols].bitcast(FP8X4),
                     lhsT_scale=wj_scales[a][:, w_cols],
                     rhs=t_codes[c][:, t_cols].bitcast(FP8X4),
@@ -215,41 +222,65 @@ def tile_inimnetdisc_pc_kernel(tc, x, w_j, b_j, w_i, out):
                     stop=(g == PASSES - 1),
                 )
 
-        def new_h_planes(c, g):
-            h_planes = stage.tile([P, PACK, CHUNK], BF16, tag="h_planes")
-            staged[("h_planes", c, g)] = h_planes
-
-        def gate_phi(c, plane, j0, j1):
+        def gatep(c, plane, j0=0, j1=None, kind="P", pair=False):
             g, t = divmod(plane, PACK)
+            w = WIDTHS[c]
+            j1 = w if j1 is None else j1
+            key = ("h", c, g)
+            if key not in staged:
+                if kind == "P":
+                    h_planes = stage.tile([P, PACK, w], BF16, tag="h_planes")
+                    staged[key] = h_planes
+                else:
+                    h_half = stage.tile([P, PACK, w], F32, tag="h_half")
+                    staged[key] = h_half
+            o0 = w if (pair and t % PAIR == 1) else 0
             nc.vector.scalar_tensor_tensor(
-                out=staged[("h_planes", c, g)][:, t, j0:j1],
-                in0=banks[("phi", c, plane)][:, j0:j1],
+                out=staged[key][:, t, j0:j1],
+                in0=banks[("phi", c, plane)][:, o0 + j0 : o0 + j1],
                 scalar=bias_bf16[:, plane : plane + 1],
                 in1=gate[c][:, plane, j0:j1],
                 op0=ALU.add,
                 op1=ALU.mult,
             )
 
-        def regroup_h(c, g, j0, j1):
+        def regroup(c, g, j0=0, j1=None):
+            j1 = WIDTHS[c] if j1 is None else j1
             h_grp = stage.tile([P, j1 - j0, PACK], BF16, tag="h_grp", align_bytes=64)
             staged[("h_grp", c, g, j0)] = h_grp
             nc.vector.tensor_copy(
                 out=h_grp[:].rearrange("q (n i) t -> q n t i", i=RUN),
-                in_=staged[("h_planes", c, g)][:, :, j0:j1].rearrange("q t (n i) -> q n t i", i=RUN),
+                in_=staged[("h", c, g)][:, :, j0:j1].rearrange("q t (n i) -> q n t i", i=RUN),
             )
 
-        def quantise_h(c, g, j0, j1):
-            h_cols = slice(g * CHUNK + j0, g * CHUNK + j1)
+        def rest(c, g, j0=0, j1=None):
+            j1 = WIDTHS[c] if j1 is None else j1
+            h_grp = stage.tile([P, j1 - j0, PACK], BF16, tag="h_grp", align_bytes=64)
+            staged[("h_grp", c, g, j0)] = h_grp
+            nc.vector.scalar_tensor_tensor(
+                out=h_grp[:],
+                in0=t_f32[c][:, planes_of(g), j0:j1].rearrange("q t n -> q n t"),
+                scalar=1.0,
+                in1=staged[("h", c, g)][:, :, j0:j1].rearrange("q t n -> q n t"),
+                op0=ALU.add,
+                op1=ALU.mult,
+            )
+
+        def qh(c, g, j0=0, j1=None):
+            w = WIDTHS[c]
+            j1 = w if j1 is None else j1
+            h_cols = slice(g * w + j0, g * w + j1)
             nc.vector.quantize_mx(
                 out=h_codes[c][:, h_cols].bitcast(FP8X4),
                 scales=h_scales[c][:, h_cols],
                 in_=staged[("h_grp", c, g, j0)][:].rearrange("q j t -> q (j t)"),
             )
 
-        def second_matmul(new_bank, c, r, s, g):
+        def mm2(c, r, s, g, new_bank=front):
             if g == 0:
                 banks[("out", c, r, s)] = new_bank()
-            h_cols = slice(g * CHUNK + r * P, g * CHUNK + (r + 1) * P)
+            w = WIDTHS[c]
+            h_cols = slice(g * w + r * P, g * w + (r + 1) * P)
             w_cols = slice(g * BANK, (g + 1) * BANK)
             nc.tensor.matmul_mx(
                 out=banks[("out", c, r, s)][:],
@@ -261,113 +292,193 @@ def tile_inimnetdisc_pc_kernel(tc, x, w_j, b_j, w_i, out):
                 stop=(g == PASSES - 1),
             )
 
-        def store(copy, c, r, s):
+        def store(c, r, s, copy):
             res = result.tile([P, BANK], F32, tag="res")
             copy(res[:], banks[("out", c, r, s)][:])
-            nc.sync.dma_start(out=out_view[c, :, r, s * BANK : (s + 1) * BANK], in_=res[:])
+            nc.sync.dma_start(out=out_view[c][:, r, s * BANK : (s + 1) * BANK], in_=res[:])
 
-        rows = range(ROW_TILES)
-        first_planes = range(PACK)
-        last_planes = range(PACK, PLANES)
-
-        transpose_x(0, 0)
-        tanh(0, 0)
-        transpose_x(0, 1)
-        tanh(0, 1)
-        transpose_wj(phi_bank, 0)
-        round_t(0, 0)
-        copy_wj(vector_copy, 0)
-        transpose_x(0, 2)
-        tanh(0, 2)
-        round_t(0, 1)
-        transpose_x(0, 3)
-        tanh(0, 3)
-        transpose_wj(phi_bank, 1)
-        round_t(0, 2)
-        quantise_wj(0)
-        transpose_wj(front_bank, 2)
-        square(0, 0)
-        round_t(0, 3)
-        quantise_t(0)
-        copy_wj(scalar_copy, 1)
-        one_minus_on_vector(0, 0)
-
-        new_h_planes(0, 0)
-        first_matmul(0, 0)
-        first_matmul(0, 1)
-        transpose_wj(front_bank, 3)
-        copy_wj(scalar_copy, 2)
-        gate_phi(0, 0, 0, CHUNK)
-        gate_phi(0, 1, 0, CHUNK)
-        quantise_wj(1)
-        first_matmul(0, 2)
-        first_matmul(0, 3)
-        copy_wj(scalar_copy, 3)
-        square(0, 1)
-        gate_phi(0, 2, 0, CHUNK)
-        gate_phi(0, 3, 0, CHUNK)
-        for r in rows:
-            transpose_x(1, r)
-            tanh(1, r)
-        quantise_wj(2)
-        quantise_wj(3)
-        regroup_h(0, 0, 0, CHUNK)
-        one_minus_on_vector(0, 1)
-        quantise_h(0, 0, 0, CHUNK)
-
-        new_h_planes(0, 1)
-        for plane in last_planes:
-            first_matmul(0, plane)
-        transpose_wi(0)
-        square(1, 0)
-        for plane in last_planes:
-            gate_phi(0, plane, 0, CHUNK)
-        regroup_h(0, 1, 0, CHUNK)
-        copy_wi(scalar_copy, 0)
-        transpose_wi(1)
-        round_t(1, 0)
-        round_t(1, 1)
-        quantise_h(0, 1, 0, CHUNK)
-        round_t(1, 2)
-        round_t(1, 3)
-        square(1, 1)
-        copy_wi(scalar_copy, 1)
-        quantise_wi(0)
-        quantise_t(1)
-        one_minus_on_vector(1, 0)
-
-        new_h_planes(1, 0)
-        for plane in first_planes:
-            first_matmul(1, plane)
-        one_minus_on_scalar(1, 1)
-        for r in rows:
-            for g in range(PASSES):
-                second_matmul(front_bank, 0, r, 0, g)
-        for plane in first_planes:
-            gate_phi(1, plane, 0, CHUNK)
-        for r in rows:
-            store(scalar_copy, 0, r, 0)
-        new_h_planes(1, 1)
-        for plane in last_planes:
-            first_matmul(1, plane)
-        regroup_h(1, 0, 0, CHUNK)
-        quantise_wi(1)
-        quantise_h(1, 0, 0, CHUNK)
-        for r in rows:
-            for g in range(PASSES):
-                second_matmul(front_bank, 0, r, 1, g)
-        for r in rows:
-            store(scalar_copy, 0, r, 1)
-
-        for j0, half_rows, new_bank in ((0, (0, 1), front_bank), (HALF, (2, 3), phi_bank)):
-            for plane in last_planes:
-                gate_phi(1, plane, j0, j0 + HALF)
-            regroup_h(1, 1, j0, j0 + HALF)
-            quantise_h(1, 1, j0, j0 + HALF)
-            for g in range(PASSES):
-                for r in half_rows:
-                    for s in range(WI_HALVES):
-                        second_matmul(new_bank, 1, r, s, g)
-            for r in half_rows:
-                store(scalar_copy if j0 == 0 else vector_copy, 1, r, 0)
-                store(scalar_copy, 1, r, 1)
+        ctx.enter_context(tc.manual_schedule())
+        load_x(0,0,1)
+        load_wj(0,0,1)
+        load_x(0,1,2)
+        load_wj(0,1,2)
+        load_x(0,2,3)
+        load_x(0,3,4)
+        load_wj(1)
+        load_wj(2)
+        load_wj(3)
+        load_bias()
+        load_wi(0,0,2)
+        load_wi(0,2,4)
+        load_x(1,0,2)
+        load_x(1,2,4)
+        load_wi(1,0,2)
+        load_wi(1,2,4)
+        nc.vector.memset(zeros[:], 0.0)
+        warm(5,phi)
+        tx(0,0)
+        tanh(0,0)
+        twj(0,0,phi)
+        tx(0,1)
+        tanh(0,1)
+        cwj(0,0,vec)
+        rnd(0,0)
+        twj(0,1,phi)
+        tx(0,2)
+        tanh(0,2)
+        cwj(0,1,vec)
+        rnd(0,1)
+        qwj(0)
+        tx(0,3)
+        tanh(0,3)
+        twj(1,0,phi)
+        twj(1,1,phi)
+        twj(2,0,phi)
+        twj(2,1,phi)
+        cwj(1,0,vec)
+        rnd(0,2)
+        cwj(1,1,sca)
+        cwj(2,0,sca)
+        rnd(0,3)
+        qt(0)
+        qwj(1)
+        cwj(2,1,sca)
+        twj(3,0)
+        twj(3,1)
+        square(0,0)
+        mm1(0,0)
+        mm1(0,1)
+        mm1(0,2)
+        mm1(0,3)
+        qwj(2)
+        om(0,0,"v")
+        twi(0,0)
+        twi(0,1)
+        cwj(3,0,sca)
+        cwj(3,1,sca)
+        gatep(0,0)
+        gatep(0,1)
+        gatep(0,2)
+        gatep(0,3)
+        square(0,1)
+        qwj(3)
+        mm1(0,4)
+        mm1(0,5)
+        twi(0,2)
+        twi(0,3)
+        mm1(0,6)
+        mm1(0,7)
+        regroup(0,0)
+        om(0,1,"v")
+        qh(0,0)
+        cwi(0,0,sca)
+        cwi(0,1,sca)
+        cwi(0,2,sca)
+        cwi(0,3,sca)
+        gatep(0,4)
+        gatep(0,5)
+        gatep(0,6)
+        gatep(0,7)
+        tx(1,0)
+        tanh(1,0)
+        tx(1,1)
+        tanh(1,1)
+        tx(1,2)
+        tanh(1,2)
+        tx(1,3)
+        tanh(1,3)
+        qwi(0)
+        regroup(0,1)
+        rnd(1,0)
+        qh(0,1)
+        rnd(1,1)
+        twi(1,0)
+        twi(1,1)
+        twi(1,2)
+        twi(1,3)
+        mm2(0,0,0,0,phi)
+        mm2(0,1,0,0,phi)
+        mm2(0,2,0,0,phi)
+        mm2(0,3,0,0,phi)
+        mm2(0,0,0,1,phi)
+        mm2(0,1,0,1,phi)
+        mm2(0,2,0,1,phi)
+        mm2(0,3,0,1,phi)
+        cwi(1,0,sca)
+        cwi(1,1,sca)
+        cwi(1,2,sca)
+        cwi(1,3,sca)
+        rnd(1,2)
+        rnd(1,3)
+        qt(1)
+        qwi(1)
+        square(1,0)
+        store(0,0,0,sca)
+        store(0,1,0,sca)
+        store(0,2,0,sca)
+        store(0,3,0,sca)
+        mm1(1,0,front)
+        mm1(1,1,front)
+        mm1(1,2,front)
+        mm1(1,3,front)
+        om(1,0,"v")
+        mm2(0,0,1,0,phi)
+        mm2(0,0,1,1,phi)
+        mm2(0,1,1,0,phi)
+        mm2(0,1,1,1,phi)
+        mm2(0,2,1,0,phi)
+        mm2(0,2,1,1,phi)
+        mm2(0,3,1,0,phi)
+        mm2(0,3,1,1,phi)
+        gatep(1,0)
+        gatep(1,1)
+        gatep(1,2)
+        gatep(1,3)
+        square(1,1)
+        om(1,1,"s")
+        mm1(1,4,front)
+        mm1(1,5,front)
+        mm1(1,6,front)
+        mm1(1,7,front)
+        regroup(1,0)
+        qh(1,0)
+        store(0,0,1,sca)
+        store(0,1,1,sca)
+        store(0,2,1,sca)
+        store(0,3,1,sca)
+        gatep(1,4,0,256)
+        gatep(1,5,0,256)
+        gatep(1,6,0,256)
+        gatep(1,7,0,256)
+        regroup(1,1,0,256)
+        qh(1,1,0,256)
+        mm2(1,0,0,0,phi)
+        mm2(1,0,1,0,phi)
+        mm2(1,1,0,0,phi)
+        mm2(1,1,1,0,phi)
+        mm2(1,0,0,1,phi)
+        mm2(1,0,1,1,phi)
+        mm2(1,1,0,1,phi)
+        mm2(1,1,1,1,phi)
+        store(1,0,0,sca)
+        store(1,0,1,sca)
+        store(1,1,0,sca)
+        store(1,1,1,sca)
+        gatep(1,4,256,512)
+        gatep(1,5,256,512)
+        gatep(1,6,256,512)
+        gatep(1,7,256,512)
+        regroup(1,1,256,512)
+        qh(1,1,256,512)
+        mm2(1,2,0,0,front)
+        mm2(1,2,1,0,front)
+        mm2(1,3,0,0,front)
+        mm2(1,3,1,0,front)
+        mm2(1,2,0,1,front)
+        mm2(1,2,1,1,front)
+        mm2(1,3,0,1,front)
+        mm2(1,3,1,1,front)
+        store(1,2,0,vec)
+        store(1,2,1,sca)
+        store(1,3,0,vec)
+        store(1,3,1,sca)

@@ -299,129 +299,139 @@ def tile_inimnetdisc_pc_kernel(tc, x, w_j, b_j, w_i, out):
 
         ctx.enter_context(tc.manual_schedule())
         load_x(0,0,1)
-        load_wj(0,0,1)
         load_x(0,1,2)
-        load_wj(0,1,2)
+        load_wj(0,0,1)
         load_x(0,2,3)
+        load_wj(0,1,2)
         load_x(0,3,4)
         load_wj(1)
         load_wj(2)
         load_wj(3)
         load_bias()
         load_wi(0,0,2)
-        load_wi(0,2,4)
         load_x(1,0,2)
+        load_wi(0,2,4)
         load_x(1,2,4)
         load_wi(1,0,2)
         load_wi(1,2,4)
         nc.vector.memset(zeros[:], 0.0)
-        warm(5,phi)
+        warm(3,phi)
         tx(0,0)
-        tanh(0,0)
-        twj(0,0,phi)
         tx(0,1)
+        twj(0,0,phi)
+        tx(0,2)
+        twj(0,1,phi)
+        tx(0,3)
+        twj(1,0,phi)
+        tanh(0,0)
         tanh(0,1)
+        tanh(0,2)
+        tanh(0,3)
         cwj(0,0,vec)
         rnd(0,0)
-        twj(0,1,phi)
-        tx(0,2)
-        tanh(0,2)
+        twj(1,1,phi)
         cwj(0,1,vec)
         rnd(0,1)
-        qwj(0)
-        tx(0,3)
-        tanh(0,3)
-        twj(1,0,phi)
-        twj(1,1,phi)
         twj(2,0,phi)
         twj(2,1,phi)
-        cwj(1,0,vec)
         rnd(0,2)
-        cwj(1,1,sca)
-        cwj(2,0,sca)
+        qwj(0)
+        cwj(1,0,sca)
+        cwj(1,1,vec)
         rnd(0,3)
-        qt(0)
         qwj(1)
-        cwj(2,1,sca)
-        twj(3,0)
-        twj(3,1)
+        qt(0)
         square(0,0)
+        cwj(2,0,sca)
+        cwj(2,1,sca)
+        twj(3,0,front)
+        twj(3,1,front)
+        cwj(3,0,sca)
+        cwj(3,1,sca)
+        twi(0,0)
+        om(0,0,"v")
+        qwj(2)
+        qwj(3)
         mm1(0,0)
         mm1(0,1)
         mm1(0,2)
         mm1(0,3)
-        qwj(2)
-        om(0,0,"v")
-        twi(0,0)
+        cwi(0,0,sca)
+        square(0,1)
+        tx(1,0)
         twi(0,1)
-        cwj(3,0,sca)
-        cwj(3,1,sca)
+        tx(1,1)
         gatep(0,0)
         gatep(0,1)
         gatep(0,2)
         gatep(0,3)
-        square(0,1)
-        qwj(3)
+        tanh(1,0)
+        cwi(0,1,sca)
         mm1(0,4)
         mm1(0,5)
         twi(0,2)
-        twi(0,3)
+        tx(1,2)
         mm1(0,6)
         mm1(0,7)
-        regroup(0,0)
-        om(0,1,"v")
-        qh(0,0)
-        cwi(0,0,sca)
-        cwi(0,1,sca)
+        twi(0,3)
+        tanh(1,1)
+        tx(1,3)
         cwi(0,2,sca)
+        om(0,1,"v")
+        regroup(0,0)
+        rnd(1,0)
+        qh(0,0)
+        tanh(1,2)
         cwi(0,3,sca)
+        tanh(1,3)
+        twi(1,0)
         gatep(0,4)
         gatep(0,5)
+        rnd(1,1)
         gatep(0,6)
         gatep(0,7)
-        tx(1,0)
-        tanh(1,0)
-        tx(1,1)
-        tanh(1,1)
-        tx(1,2)
-        tanh(1,2)
-        tx(1,3)
-        tanh(1,3)
-        qwi(0)
-        regroup(0,1)
-        rnd(1,0)
-        qh(0,1)
-        rnd(1,1)
-        twi(1,0)
+        cwi(1,0,sca)
+        square(1,0)
         twi(1,1)
         twi(1,2)
         twi(1,3)
+        qwi(0)
+        regroup(0,1)
+        rnd(1,2)
+        rnd(1,3)
+        qh(0,1)
         mm2(0,0,0,0,phi)
         mm2(0,1,0,0,phi)
         mm2(0,2,0,0,phi)
         mm2(0,3,0,0,phi)
+        cwi(1,1,sca)
+        cwi(1,2,sca)
+        cwi(1,3,sca)
+        square(1,1)
         mm2(0,0,0,1,phi)
         mm2(0,1,0,1,phi)
         mm2(0,2,0,1,phi)
         mm2(0,3,0,1,phi)
-        cwi(1,0,sca)
-        cwi(1,1,sca)
-        cwi(1,2,sca)
-        cwi(1,3,sca)
-        rnd(1,2)
-        rnd(1,3)
         qt(1)
+        om(1,0,"v")
         qwi(1)
-        square(1,0)
-        store(0,0,0,sca)
-        store(0,1,0,sca)
-        store(0,2,0,sca)
-        store(0,3,0,sca)
         mm1(1,0,front)
         mm1(1,1,front)
         mm1(1,2,front)
         mm1(1,3,front)
-        om(1,0,"v")
+        om(1,1,"s")
+        store(0,0,0,sca)
+        store(0,1,0,sca)
+        store(0,2,0,sca)
+        store(0,3,0,sca)
+        gatep(1,0)
+        gatep(1,1)
+        gatep(1,2)
+        gatep(1,3)
+        mm1(1,4,front)
+        mm1(1,5,front)
+        mm1(1,6,front)
+        mm1(1,7,front)
         mm2(0,0,1,0,phi)
         mm2(0,0,1,1,phi)
         mm2(0,1,1,0,phi)
@@ -430,53 +440,47 @@ def tile_inimnetdisc_pc_kernel(tc, x, w_j, b_j, w_i, out):
         mm2(0,2,1,1,phi)
         mm2(0,3,1,0,phi)
         mm2(0,3,1,1,phi)
-        gatep(1,0)
-        gatep(1,1)
-        gatep(1,2)
-        gatep(1,3)
-        square(1,1)
-        om(1,1,"s")
-        mm1(1,4,front)
-        mm1(1,5,front)
-        mm1(1,6,front)
-        mm1(1,7,front)
-        regroup(1,0)
-        qh(1,0)
         store(0,0,1,sca)
         store(0,1,1,sca)
         store(0,2,1,sca)
         store(0,3,1,sca)
         gatep(1,4,0,256)
+        regroup(1,0,0,256)
         gatep(1,5,0,256)
         gatep(1,6,0,256)
+        qh(1,0,0,256)
         gatep(1,7,0,256)
+        regroup(1,0,256,512)
         regroup(1,1,0,256)
+        gatep(1,4,256,512)
         qh(1,1,0,256)
+        gatep(1,5,256,512)
+        qh(1,0,256,512)
+        gatep(1,6,256,512)
+        gatep(1,7,256,512)
         mm2(1,0,0,0,phi)
-        mm2(1,0,1,0,phi)
-        mm2(1,1,0,0,phi)
-        mm2(1,1,1,0,phi)
         mm2(1,0,0,1,phi)
+        mm2(1,0,1,0,phi)
         mm2(1,0,1,1,phi)
+        mm2(1,1,0,0,phi)
         mm2(1,1,0,1,phi)
+        mm2(1,1,1,0,phi)
         mm2(1,1,1,1,phi)
         store(1,0,0,sca)
         store(1,0,1,sca)
         store(1,1,0,sca)
         store(1,1,1,sca)
-        gatep(1,4,256,512)
-        gatep(1,5,256,512)
-        gatep(1,6,256,512)
-        gatep(1,7,256,512)
-        regroup(1,1,256,512)
-        qh(1,1,256,512)
+        regroup(1,1,256,384)
+        regroup(1,1,384,512)
+        qh(1,1,256,384)
+        qh(1,1,384,512)
         mm2(1,2,0,0,front)
-        mm2(1,2,1,0,front)
-        mm2(1,3,0,0,front)
-        mm2(1,3,1,0,front)
         mm2(1,2,0,1,front)
+        mm2(1,2,1,0,front)
         mm2(1,2,1,1,front)
+        mm2(1,3,0,0,front)
         mm2(1,3,0,1,front)
+        mm2(1,3,1,0,front)
         mm2(1,3,1,1,front)
         store(1,2,0,vec)
         store(1,2,1,sca)

@@ -191,6 +191,22 @@ def tile_inimnetdisc_pc_kernel(tc, x, w_j, b_j, w_i, out):
             else:
                 nc.scalar.activation(out=dst, in_=dst, func=ACT.Copy, scale=-1.0, bias=1.0)
 
+        def omp(c, p0, p1, eng):
+            dst = gate[c][:, p0:p1, :]
+            if eng == "v":
+                nc.vector.tensor_scalar(out=dst, in0=dst, scalar1=-1.0, scalar2=1.0, op0=ALU.mult, op1=ALU.add)
+            elif eng == "g":
+                nc.gpsimd.tensor_scalar(out=dst, in0=dst, scalar1=-1.0, scalar2=1.0, op0=ALU.mult, op1=ALU.add)
+            else:
+                nc.scalar.activation(out=dst, in_=dst, func=ACT.Copy, scale=-1.0, bias=1.0)
+
+        def rnd2(c, r0, g):
+            cols = slice(r0 * P, (r0 + 2) * P)
+            nc.vector.tensor_copy(
+                out=t_grp[c][:, g, cols, :].rearrange("q (n i) t -> q n t i", i=RUN),
+                in_=t_f32[c][:, planes_of(g), cols].rearrange("q t (n i) -> q n t i", i=RUN),
+            )
+
         def less(c, g, eng):
             dst = gate[c][:, planes_of(g), :]
             src = t_f32[c][:, planes_of(g), :]
@@ -379,15 +395,15 @@ def tile_inimnetdisc_pc_kernel(tc, x, w_j, b_j, w_i, out):
         cwi(0,2,sca)
         om(0,1,"v")
         regroup(0,0)
-        rnd(1,0)
+        gatep(0,4)
         qh(0,0)
         tanh(1,2)
         cwi(0,3,sca)
         tanh(1,3)
         twi(1,0)
-        gatep(0,4)
+        rnd2(1,0,0)
         gatep(0,5)
-        rnd(1,1)
+        rnd2(1,0,1)
         gatep(0,6)
         gatep(0,7)
         cwi(1,0,sca)
@@ -397,8 +413,8 @@ def tile_inimnetdisc_pc_kernel(tc, x, w_j, b_j, w_i, out):
         twi(1,3)
         qwi(0)
         regroup(0,1)
-        rnd(1,2)
-        rnd(1,3)
+        rnd2(1,2,0)
+        rnd2(1,2,1)
         qh(0,1)
         mm2(0,0,0,0,phi)
         mm2(0,1,0,0,phi)

@@ -200,8 +200,8 @@ def tile_inimnetdisc_pc_kernel(tc, x, w_j, b_j, w_i, out):
             else:
                 nc.scalar.activation(out=dst, in_=dst, func=ACT.Copy, scale=-1.0, bias=1.0)
 
-        def rnd2(c, r0, g):
-            cols = slice(r0 * P, (r0 + 2) * P)
+        def rnd2(c, r0, g, n=2):
+            cols = slice(r0 * P, (r0 + n) * P)
             nc.vector.tensor_copy(
                 out=t_grp[c][:, g, cols, :].rearrange("q (n i) t -> q n t i", i=RUN),
                 in_=t_f32[c][:, planes_of(g), cols].rearrange("q t (n i) -> q n t i", i=RUN),
@@ -344,17 +344,21 @@ def tile_inimnetdisc_pc_kernel(tc, x, w_j, b_j, w_i, out):
         tanh(0,2)
         tanh(0,3)
         cwj(0,0,vec)
-        rnd(0,0)
         twj(1,1,phi)
+        rnd2(0,0,0,1)
+        rnd2(0,0,1,1)
         cwj(0,1,vec)
-        rnd(0,1)
+        rnd2(0,1,0,1)
+        rnd2(0,1,1,1)
         twj(2,0,phi)
         twj(2,1,phi)
-        rnd(0,2)
+        rnd2(0,2,0,1)
+        rnd2(0,2,1,1)
         qwj(0)
         cwj(1,0,sca)
         cwj(1,1,vec)
-        rnd(0,3)
+        rnd2(0,3,0,1)
+        rnd2(0,3,1,1)
         qwj(1)
         qt(0)
         square(0,0)

@@ -109,18 +109,47 @@ def tile_inimnetdisc_pc_kernel(tc, x, w_j, b_j, w_i, out):
                 in_=b_j.rearrange("(a q e) -> q a e", q=P, e=PAIR),
             )
 
-        def transpose_words(new_bank, key, rows):
+        def transpose_words(new_bank, key, rows, dummies=0):
             banks[key] = new_bank()
+            for i in range(dummies):
+                nc.tensor.matmul(banks[key][:], lhsT=zeros[:, :P], rhs=zeros[:], start=True, stop=True)
             words = rows.bitcast(F32)
             for v in range(WORD_BLOCKS):
                 block = slice(v * P, (v + 1) * P)
                 nc.tensor.transpose(banks[key][:, block], words[:, block], ident[:])
 
-        def tx(c, r, new_bank=front):
-            transpose_words(new_bank, ("x", c, r), x_sb[c][:, r, :])
+        def tx(c, r, new_bank=front, dummies=0):
+            transpose_words(new_bank, ("x", c, r), x_sb[c][:, r, :], dummies)
 
-        def twj(a, e, new_bank=front):
-            transpose_words(new_bank, ("wj", a, e), wj_sb[a][:, e, :])
+        def load_xh(c, r, h):
+            cols = slice(h * BANK, (h + 1) * BANK)
+            nc.sync.dma_start(out=x_sb[c][:, r, cols], in_=x_view[c][:, r, cols])
+
+        def txh(c, r, h, new_bank=front):
+            if h == 0:
+                banks[("x", c, r)] = new_bank()
+            words = x_sb[c][:, r, :].bitcast(F32)
+            for v in (2 * h, 2 * h + 1):
+                block = slice(v * P, (v + 1) * P)
+                nc.tensor.transpose(banks[("x", c, r)][:, block], words[:, block], ident[:])
+
+        def tanhh(c, r, h):
+            cols = slice(r * P, (r + 1) * P)
+            half = slice(h * 2 * P, (h + 1) * 2 * P)
+            nc.scalar.activation(
+                out=t_f32[c][:, h * PACK : (h + 1) * PACK, cols].rearrange("q (v e) p -> q v e p", e=PAIR),
+                in_=banks[("x", c, r)][:, half].bitcast(BF16).rearrange("q (v p e) -> q v e p", v=2, e=PAIR),
+                func=ACT.Tanh,
+            )
+
+        def storeh(c, r, s, h, copy):
+            cols = slice(h * BANK // 2, (h + 1) * BANK // 2)
+            res = result.tile([P, BANK // 2], F32, tag="resh")
+            copy(res[:], banks[("out", c, r, s)][:, cols])
+            nc.sync.dma_start(out=out_view[c][:, r, s * BANK + h * BANK // 2 : s * BANK + (h + 1) * BANK // 2], in_=res[:])
+
+        def twj(a, e, new_bank=front, dummies=0):
+            transpose_words(new_bank, ("wj", a, e), wj_sb[a][:, e, :], dummies)
 
         def twi(s, m, new_bank=front):
             transpose_words(new_bank, ("wi", s, m), wi_sb[s][:, m, :])
@@ -200,11 +229,11 @@ def tile_inimnetdisc_pc_kernel(tc, x, w_j, b_j, w_i, out):
             else:
                 nc.scalar.activation(out=dst, in_=dst, func=ACT.Copy, scale=-1.0, bias=1.0)
 
-        def rnd2(c, r0, g, n=2):
+        def rnd2(c, r0, g, n=2, eng="v"):
             cols = slice(r0 * P, (r0 + n) * P)
-            nc.vector.tensor_copy(
-                out=t_grp[c][:, g, cols, :].rearrange("q (n i) t -> q n t i", i=RUN),
-                in_=t_f32[c][:, planes_of(g), cols].rearrange("q t (n i) -> q n t i", i=RUN),
+            (vec if eng == "v" else sca)(
+                out_ap=t_grp[c][:, g, cols, :].rearrange("q (n i) t -> q n t i", i=RUN),
+                in_ap=t_f32[c][:, planes_of(g), cols].rearrange("q t (n i) -> q n t i", i=RUN),
             )
 
         def less(c, g, eng):
@@ -260,13 +289,13 @@ def tile_inimnetdisc_pc_kernel(tc, x, w_j, b_j, w_i, out):
                 op1=ALU.mult,
             )
 
-        def regroup(c, g, j0=0, j1=None):
+        def regroup(c, g, j0=0, j1=None, eng="v"):
             j1 = WIDTHS[c] if j1 is None else j1
             h_grp = stage.tile([P, j1 - j0, PACK], BF16, tag="h_grp", align_bytes=64)
             staged[("h_grp", c, g, j0)] = h_grp
-            nc.vector.tensor_copy(
-                out=h_grp[:].rearrange("q (n i) t -> q n t i", i=RUN),
-                in_=staged[("h", c, g)][:, :, j0:j1].rearrange("q t (n i) -> q n t i", i=RUN),
+            (vec if eng == "v" else sca)(
+                out_ap=h_grp[:].rearrange("q (n i) t -> q n t i", i=RUN),
+                in_ap=staged[("h", c, g)][:, :, j0:j1].rearrange("q t (n i) -> q n t i", i=RUN),
             )
 
         def rest(c, g, j0=0, j1=None):
@@ -405,7 +434,7 @@ def tile_inimnetdisc_pc_kernel(tc, x, w_j, b_j, w_i, out):
         cwi(0,3,sca)
         tanh(1,3)
         twi(1,0)
-        rnd2(1,0,0)
+        rnd2(1,0,0,2,"s")
         gatep(0,5)
         rnd2(1,0,1)
         gatep(0,6)
@@ -468,16 +497,16 @@ def tile_inimnetdisc_pc_kernel(tc, x, w_j, b_j, w_i, out):
         regroup(1,0,0,256)
         gatep(1,5,0,256)
         gatep(1,6,0,256)
-        qh(1,0,0,256)
         gatep(1,7,0,256)
-        regroup(1,0,256,512)
+        qh(1,0,0,256)
         regroup(1,1,0,256)
         gatep(1,4,256,512)
         qh(1,1,0,256)
+        regroup(1,0,256,512)
         gatep(1,5,256,512)
-        qh(1,0,256,512)
         gatep(1,6,256,512)
         gatep(1,7,256,512)
+        qh(1,0,256,512)
         mm2(1,0,0,0,phi)
         mm2(1,0,0,1,phi)
         mm2(1,0,1,0,phi)

@@ -25,6 +25,7 @@ WJ_BLOCKS = D // (PAIR * P)
 WI_HALVES = D // BANK
 ROW_TILES = BANK // P
 RUN = 4
+HRUN = 4
 WIDTHS = (512, 512)
 STARTS = [sum(WIDTHS[:c]) for c in range(len(WIDTHS))]
 CHUNKS = len(WIDTHS)
@@ -37,7 +38,8 @@ def tile_inimnetdisc_pc_kernel(tc, x, w_j, b_j, w_i, out):
         keep = ctx.enter_context(tc.tile_pool(name="keep", bufs=1))
         wj_stage = ctx.enter_context(tc.tile_pool(name="wj_stage", bufs=4))
         stage = ctx.enter_context(tc.tile_pool(name="stage", bufs=2))
-        result = ctx.enter_context(tc.tile_pool(name="result", bufs=6))
+        h_stage = ctx.enter_context(tc.tile_pool(name="h_stage", bufs=2))
+        result = ctx.enter_context(tc.tile_pool(name="result", bufs=10))
         front_psum = ctx.enter_context(tc.psum_pool(name="front_psum", bufs=4))
         phi_psum = ctx.enter_context(tc.psum_pool(name="phi_psum", bufs=4))
 
@@ -121,33 +123,6 @@ def tile_inimnetdisc_pc_kernel(tc, x, w_j, b_j, w_i, out):
         def tx(c, r, new_bank=front, dummies=0):
             transpose_words(new_bank, ("x", c, r), x_sb[c][:, r, :], dummies)
 
-        def load_xh(c, r, h):
-            cols = slice(h * BANK, (h + 1) * BANK)
-            nc.sync.dma_start(out=x_sb[c][:, r, cols], in_=x_view[c][:, r, cols])
-
-        def txh(c, r, h, new_bank=front):
-            if h == 0:
-                banks[("x", c, r)] = new_bank()
-            words = x_sb[c][:, r, :].bitcast(F32)
-            for v in (2 * h, 2 * h + 1):
-                block = slice(v * P, (v + 1) * P)
-                nc.tensor.transpose(banks[("x", c, r)][:, block], words[:, block], ident[:])
-
-        def tanhh(c, r, h):
-            cols = slice(r * P, (r + 1) * P)
-            half = slice(h * 2 * P, (h + 1) * 2 * P)
-            nc.scalar.activation(
-                out=t_f32[c][:, h * PACK : (h + 1) * PACK, cols].rearrange("q (v e) p -> q v e p", e=PAIR),
-                in_=banks[("x", c, r)][:, half].bitcast(BF16).rearrange("q (v p e) -> q v e p", v=2, e=PAIR),
-                func=ACT.Tanh,
-            )
-
-        def storeh(c, r, s, h, copy):
-            cols = slice(h * BANK // 2, (h + 1) * BANK // 2)
-            res = result.tile([P, BANK // 2], F32, tag="resh")
-            copy(res[:], banks[("out", c, r, s)][:, cols])
-            nc.sync.dma_start(out=out_view[c][:, r, s * BANK + h * BANK // 2 : s * BANK + (h + 1) * BANK // 2], in_=res[:])
-
         def twj(a, e, new_bank=front, dummies=0):
             transpose_words(new_bank, ("wj", a, e), wj_sb[a][:, e, :], dummies)
 
@@ -160,13 +135,6 @@ def tile_inimnetdisc_pc_kernel(tc, x, w_j, b_j, w_i, out):
                 out=t_f32[c][:, :, cols].rearrange("q (v e) p -> q v e p", e=PAIR),
                 in_=banks[("x", c, r)][:].bitcast(BF16).rearrange("q (v p e) -> q v e p", v=WORD_BLOCKS, e=PAIR),
                 func=ACT.Tanh,
-            )
-
-        def rnd(c, r):
-            cols = slice(r * P, (r + 1) * P)
-            nc.vector.tensor_copy(
-                out=t_grp[c][:, :, cols, :],
-                in_=t_f32[c][:, :, cols].rearrange("q (g t) j -> q g j t", t=PACK),
             )
 
         def qt(c):
@@ -236,16 +204,6 @@ def tile_inimnetdisc_pc_kernel(tc, x, w_j, b_j, w_i, out):
                 in_ap=t_f32[c][:, planes_of(g), cols].rearrange("q t (n i) -> q n t i", i=RUN),
             )
 
-        def less(c, g, eng):
-            dst = gate[c][:, planes_of(g), :]
-            src = t_f32[c][:, planes_of(g), :]
-            if eng == "v":
-                nc.vector.tensor_scalar(out=dst, in0=src, scalar1=-1.0, scalar2=1.0, op0=ALU.mult, op1=ALU.add)
-            elif eng == "g":
-                nc.gpsimd.tensor_scalar(out=dst, in0=src, scalar1=-1.0, scalar2=1.0, op0=ALU.mult, op1=ALU.add)
-            else:
-                nc.scalar.activation(out=dst, in_=src, func=ACT.Copy, scale=-1.0, bias=1.0)
-
         def mm1(c, plane, new_bank=phi, pair=False):
             a, e = divmod(plane, PAIR)
             w = WIDTHS[c]
@@ -291,24 +249,11 @@ def tile_inimnetdisc_pc_kernel(tc, x, w_j, b_j, w_i, out):
 
         def regroup(c, g, j0=0, j1=None, eng="v"):
             j1 = WIDTHS[c] if j1 is None else j1
-            h_grp = stage.tile([P, j1 - j0, PACK], BF16, tag="h_grp", align_bytes=64)
+            h_grp = h_stage.tile([P, j1 - j0, PACK], BF16, tag="h_grp", align_bytes=64)
             staged[("h_grp", c, g, j0)] = h_grp
             (vec if eng == "v" else sca)(
-                out_ap=h_grp[:].rearrange("q (n i) t -> q n t i", i=RUN),
-                in_ap=staged[("h", c, g)][:, :, j0:j1].rearrange("q t (n i) -> q n t i", i=RUN),
-            )
-
-        def rest(c, g, j0=0, j1=None):
-            j1 = WIDTHS[c] if j1 is None else j1
-            h_grp = stage.tile([P, j1 - j0, PACK], BF16, tag="h_grp", align_bytes=64)
-            staged[("h_grp", c, g, j0)] = h_grp
-            nc.vector.scalar_tensor_tensor(
-                out=h_grp[:],
-                in0=t_f32[c][:, planes_of(g), j0:j1].rearrange("q t n -> q n t"),
-                scalar=1.0,
-                in1=staged[("h", c, g)][:, :, j0:j1].rearrange("q t n -> q n t"),
-                op0=ALU.add,
-                op1=ALU.mult,
+                out_ap=h_grp[:].rearrange("q (n i) t -> q n t i", i=HRUN),
+                in_ap=staged[("h", c, g)][:, :, j0:j1].rearrange("q t (n i) -> q n t i", i=HRUN),
             )
 
         def qh(c, g, j0=0, j1=None):
@@ -468,10 +413,11 @@ def tile_inimnetdisc_pc_kernel(tc, x, w_j, b_j, w_i, out):
         mm1(1,1,front)
         mm1(1,2,front)
         mm1(1,3,front)
-        om(1,1,"s")
         store(0,0,0,sca)
+        omp(1,4,6,"s")
         store(0,1,0,sca)
         store(0,2,0,sca)
+        omp(1,6,8,"s")
         store(0,3,0,sca)
         gatep(1,0)
         gatep(1,1)
@@ -520,8 +466,8 @@ def tile_inimnetdisc_pc_kernel(tc, x, w_j, b_j, w_i, out):
         store(1,1,0,sca)
         store(1,1,1,sca)
         regroup(1,1,256,384)
-        regroup(1,1,384,512)
         qh(1,1,256,384)
+        regroup(1,1,384,512)
         qh(1,1,384,512)
         mm2(1,2,0,0,front)
         mm2(1,2,0,1,front)

from contextlib import ExitStack

import concourse.mybir as mybir
from concourse.masks import make_identity

F32 = mybir.dt.float32
BF16 = mybir.dt.bfloat16
U32 = mybir.dt.uint32
U8 = mybir.dt.uint8
FP8X4 = mybir.dt.float8_e4m3fn_x4
ACT = mybir.ActivationFunctionType
ALU = mybir.AluOpType

P = 128
B = 1024
D = 1024
PACK = 4
K_PASS = P * PACK
PASSES = D // K_PASS
BANK = 512
PLANES = D // P
PAIR = 2
WORD_BLOCKS = D // (PAIR * P)
WJ_BLOCKS = D // (PAIR * P)
WI_HALVES = D // BANK
ROW_TILES = BANK // P
RUN = 4
HRUN = 4
WIDTHS = (512, 512)
STARTS = [sum(WIDTHS[:c]) for c in range(len(WIDTHS))]
CHUNKS = len(WIDTHS)
FLOPS = 2 * 2 * B * D * D


def tile_inimnetdisc_pc_kernel(tc, x, w_j, b_j, w_i, out):
    nc = tc.nc
    with ExitStack() as ctx:
        keep = ctx.enter_context(tc.tile_pool(name="keep", bufs=1))
        wj_stage = ctx.enter_context(tc.tile_pool(name="wj_stage", bufs=4))
        stage = ctx.enter_context(tc.tile_pool(name="stage", bufs=2))
        h_stage = ctx.enter_context(tc.tile_pool(name="h_stage", bufs=2))
        result = ctx.enter_context(tc.tile_pool(name="result", bufs=10))
        front_psum = ctx.enter_context(tc.psum_pool(name="front_psum", bufs=4))
        phi_psum = ctx.enter_context(tc.psum_pool(name="phi_psum", bufs=4))

        def rows_view(dram, c):
            part = dram[STARTS[c] : STARTS[c] + WIDTHS[c], :]
            return part.rearrange("(p r) k -> p r k", p=P)

        x_view = [rows_view(x, c) for c in range(CHUNKS)]
        out_view = [rows_view(out, c) for c in range(CHUNKS)]
        wj_view = w_j.rearrange("(a p e) k -> a p e k", p=P, e=PAIR)
        wi_view = w_i.rearrange("(s m p) k -> s p m k", m=ROW_TILES, p=P)

        x_sb = [keep.tile([P, WIDTHS[c] // P, D], BF16, name="x_sb%d" % c) for c in range(CHUNKS)]
        wj_sb = [keep.tile([P, PAIR, D], BF16, name="wj_sb%d" % a) for a in range(WJ_BLOCKS)]
        wi_sb = [keep.tile([P, ROW_TILES, D], BF16, name="wi_sb%d" % s) for s in range(WI_HALVES)]
        t_f32 = [keep.tile([P, PLANES, WIDTHS[c]], F32, name="t_f32_%d" % c) for c in range(CHUNKS)]
        gate = [keep.tile([P, PLANES, WIDTHS[c]], F32, name="gate%d" % c) for c in range(CHUNKS)]
        t_grp = [keep.tile([P, PASSES, WIDTHS[c], PACK], BF16, name="t_grp%d" % c, align_bytes=64) for c in range(CHUNKS)]

        def quantised(name, words_of):
            codes = [keep.tile([P, w], U32, name="%s_codes%d" % (name, i), align_bytes=64) for i, w in enumerate(words_of)]
            scales = [keep.tile([P, w], U8, name="%s_scales%d" % (name, i), align_bytes=64) for i, w in enumerate(words_of)]
            return codes, scales

        t_codes, t_scales = quantised("t", [PASSES * w for w in WIDTHS])
        h_codes, h_scales = quantised("h", [PASSES * w for w in WIDTHS])
        wj_codes, wj_scales = quantised("wj", [PASSES * PAIR * P] * WJ_BLOCKS)
        wi_codes, wi_scales = quantised("wi", [PASSES * BANK] * WI_HALVES)

        ident = keep.tile([P, P], F32, name="ident")
        make_identity(nc, ident[:])
        bias_bf16 = keep.tile([P, PLANES], BF16, name="bias_bf16")

        banks = {}
        staged = {}
        zeros = keep.tile([P, BANK], BF16, name="zeros")

        def warm(n, new_bank):
            bank = new_bank()
            for i in range(n):
                nc.tensor.matmul(bank[:], lhsT=zeros[:, :P], rhs=zeros[:], start=True, stop=True)

        def front():
            bank = front_psum.tile([P, BANK], F32, tag="front")
            return bank

        def phi():
            bank = phi_psum.tile([P, BANK], F32, tag="phi")
            return bank

        def vec(out_ap, in_ap):
            nc.vector.tensor_copy(out=out_ap, in_=in_ap)

        def sca(out_ap, in_ap):
            nc.scalar.copy(out=out_ap, in_=in_ap)

        def load_x(c, r0, r1):
            nc.sync.dma_start(out=x_sb[c][:, r0:r1, :], in_=x_view[c][:, r0:r1, :])

        def load_wj(a, e0=0, e1=PAIR):
            nc.sync.dma_start(out=wj_sb[a][:, e0:e1, :], in_=wj_view[a][:, e0:e1, :])

        def load_wi(s, m0, m1):
            nc.sync.dma_start(out=wi_sb[s][:, m0:m1, :], in_=wi_view[s][:, m0:m1, :])

        def load_bias():
            nc.sync.dma_start(
                out=bias_bf16[:].rearrange("q (a e) -> q a e", e=PAIR),
                in_=b_j.rearrange("(a q e) -> q a e", q=P, e=PAIR),
            )

        def transpose_words(new_bank, key, rows, dummies=0):
            banks[key] = new_bank()
            for i in range(dummies):
                nc.tensor.matmul(banks[key][:], lhsT=zeros[:, :P], rhs=zeros[:], start=True, stop=True)
            words = rows.bitcast(F32)
            for v in range(WORD_BLOCKS):
                block = slice(v * P, (v + 1) * P)
                nc.tensor.transpose(banks[key][:, block], words[:, block], ident[:])

        def tx(c, r, new_bank=front, dummies=0):
            transpose_words(new_bank, ("x", c, r), x_sb[c][:, r, :], dummies)

        def twj(a, e, new_bank=front, dummies=0):
            transpose_words(new_bank, ("wj", a, e), wj_sb[a][:, e, :], dummies)

        def twi(s, m, new_bank=front):
            transpose_words(new_bank, ("wi", s, m), wi_sb[s][:, m, :])

        def tanh(c, r):
            cols = slice(r * P, (r + 1) * P)
            nc.scalar.activation(
                out=t_f32[c][:, :, cols].rearrange("q (v e) p -> q v e p", e=PAIR),
                in_=banks[("x", c, r)][:].bitcast(BF16).rearrange("q (v p e) -> q v e p", v=WORD_BLOCKS, e=PAIR),
                func=ACT.Tanh,
            )

        def qt(c):
            nc.vector.quantize_mx(
                out=t_codes[c][:].bitcast(FP8X4),
                scales=t_scales[c][:],
                in_=t_grp[c][:].rearrange("q g j t -> q (g j t)"),
            )

        def words_by_pass(bank):
            return bank[:].rearrange("q (g u p) -> q g p u", g=PASSES, u=PAIR)

        def cwj(a, e, copy):
            if e == 0:
                wj_grp = wj_stage.tile([P, PASSES * PAIR * P * PACK], BF16, tag="wj_grp", align_bytes=64)
                staged[("wj", a)] = wj_grp
            grp_words = staged[("wj", a)][:].bitcast(F32).rearrange("q (g e p u) -> q g e p u", g=PASSES, e=PAIR, u=PAIR)
            copy(grp_words[:, :, e, :, :], words_by_pass(banks[("wj", a, e)]))

        def qwj(a):
            nc.vector.quantize_mx(
                out=wj_codes[a][:].bitcast(FP8X4), scales=wj_scales[a][:], in_=staged[("wj", a)][:]
            )

        def cwi(s, m, copy):
            if m == 0:
                wi_grp = stage.tile([P, PASSES * BANK * PACK], BF16, tag="wi_grp", align_bytes=64)
                staged[("wi", s)] = wi_grp
            grp_words = staged[("wi", s)][:].bitcast(F32).rearrange("q (g m p u) -> q g m p u", g=PASSES, m=ROW_TILES, u=PAIR)
            copy(grp_words[:, :, m, :, :], words_by_pass(banks[("wi", s, m)]))

        def qwi(s, g0=0, g1=PASSES):
            words = slice(g0 * BANK, g1 * BANK)
            nc.vector.quantize_mx(
                out=wi_codes[s][:, words].bitcast(FP8X4), scales=wi_scales[s][:, words],
                in_=staged[("wi", s)][:, g0 * BANK * PACK : g1 * BANK * PACK],
            )

        def planes_of(g):
            return slice(g * PACK, (g + 1) * PACK)

        def square(c, g):
            nc.scalar.activation(out=gate[c][:, planes_of(g), :], in_=t_f32[c][:, planes_of(g), :], func=ACT.Square)

        def om(c, g, eng):
            dst = gate[c][:, planes_of(g), :]
            if eng == "v":
                nc.vector.tensor_scalar(out=dst, in0=dst, scalar1=-1.0, scalar2=1.0, op0=ALU.mult, op1=ALU.add)
            elif eng == "g":
                nc.gpsimd.tensor_scalar(out=dst, in0=dst, scalar1=-1.0, scalar2=1.0, op0=ALU.mult, op1=ALU.add)
            else:
                nc.scalar.activation(out=dst, in_=dst, func=ACT.Copy, scale=-1.0, bias=1.0)

        def omp(c, p0, p1, eng):
            dst = gate[c][:, p0:p1, :]
            if eng == "v":
                nc.vector.tensor_scalar(out=dst, in0=dst, scalar1=-1.0, scalar2=1.0, op0=ALU.mult, op1=ALU.add)
            elif eng == "g":
                nc.gpsimd.tensor_scalar(out=dst, in0=dst, scalar1=-1.0, scalar2=1.0, op0=ALU.mult, op1=ALU.add)
            else:
                nc.scalar.activation(out=dst, in_=dst, func=ACT.Copy, scale=-1.0, bias=1.0)

        def rnd2(c, r0, g, n=2, eng="v"):
            cols = slice(r0 * P, (r0 + n) * P)
            (vec if eng == "v" else sca)(
                out_ap=t_grp[c][:, g, cols, :].rearrange("q (n i) t -> q n t i", i=RUN),
                in_ap=t_f32[c][:, planes_of(g), cols].rearrange("q t (n i) -> q n t i", i=RUN),
            )

        def mm1(c, plane, new_bank=phi, pair=False):
            a, e = divmod(plane, PAIR)
            w = WIDTHS[c]
            if not pair or e == 0:
                banks[("phi", c, plane)] = new_bank()
            else:
                banks[("phi", c, plane)] = banks[("phi", c, plane - 1)]
            o0 = w if (pair and e == 1) else 0
            for g in range(PASSES):
                w_cols = slice((g * PAIR + e) * P, (g * PAIR + e + 1) * P)
                t_cols = slice(g * w, (g + 1) * w)
                nc.tensor.matmul_mx(
                    out=banks[("phi", c, plane)][:, o0 : o0 + w],
                    lhsT=wj_codes[a][:, w_cols].bitcast(FP8X4),
                    lhsT_scale=wj_scales[a][:, w_cols],
                    rhs=t_codes[c][:, t_cols].bitcast(FP8X4),
                    rhs_scale=t_scales[c][:, t_cols],
                    start=(g == 0),
                    stop=(g == PASSES - 1),
                )

        def gatep(c, plane, j0=0, j1=None, kind="P", pair=False):
            g, t = divmod(plane, PACK)
            w = WIDTHS[c]
            j1 = w if j1 is None else j1
            key = ("h", c, g)
            if key not in staged:
                if kind == "P":
                    h_planes = stage.tile([P, PACK, w], BF16, tag="h_planes")
                    staged[key] = h_planes
                else:
                    h_half = stage.tile([P, PACK, w], F32, tag="h_half")
                    staged[key] = h_half
            o0 = w if (pair and t % PAIR == 1) else 0
            nc.vector.scalar_tensor_tensor(
                out=staged[key][:, t, j0:j1],
                in0=banks[("phi", c, plane)][:, o0 + j0 : o0 + j1],
                scalar=bias_bf16[:, plane : plane + 1],
                in1=gate[c][:, plane, j0:j1],
                op0=ALU.add,
                op1=ALU.mult,
            )

        def regroup(c, g, j0=0, j1=None, eng="v"):
            j1 = WIDTHS[c] if j1 is None else j1
            h_grp = h_stage.tile([P, j1 - j0, PACK], BF16, tag="h_grp", align_bytes=64)
            staged[("h_grp", c, g, j0)] = h_grp
            (vec if eng == "v" else sca)(
                out_ap=h_grp[:].rearrange("q (n i) t -> q n t i", i=HRUN),
                in_ap=staged[("h", c, g)][:, :, j0:j1].rearrange("q t (n i) -> q n t i", i=HRUN),
            )

        def qh(c, g, j0=0, j1=None):
            w = WIDTHS[c]
            j1 = w if j1 is None else j1
            h_cols = slice(g * w + j0, g * w + j1)
            nc.vector.quantize_mx(
                out=h_codes[c][:, h_cols].bitcast(FP8X4),
                scales=h_scales[c][:, h_cols],
                in_=staged[("h_grp", c, g, j0)][:].rearrange("q j t -> q (j t)"),
            )

        def mm2(c, r, s, g, new_bank=front):
            if g == 0:
                banks[("out", c, r, s)] = new_bank()
            w = WIDTHS[c]
            h_cols = slice(g * w + r * P, g * w + (r + 1) * P)
            w_cols = slice(g * BANK, (g + 1) * BANK)
            nc.tensor.matmul_mx(
                out=banks[("out", c, r, s)][:],
                lhsT=h_codes[c][:, h_cols].bitcast(FP8X4),
                lhsT_scale=h_scales[c][:, h_cols],
                rhs=wi_codes[s][:, w_cols].bitcast(FP8X4),
                rhs_scale=wi_scales[s][:, w_cols],
                start=(g == 0),
                stop=(g == PASSES - 1),
            )

        def store(c, r, s, copy):
            res = result.tile([P, BANK], F32, tag="res")
            copy(res[:], banks[("out", c, r, s)][:])
            nc.sync.dma_start(out=out_view[c][:, r, s * BANK : (s + 1) * BANK], in_=res[:])

        ctx.enter_context(tc.manual_schedule())
        load_x(0,0,1)
        load_x(0,1,2)
        load_wj(0,0,1)
        load_x(0,2,3)
        load_wj(0,1,2)
        load_x(0,3,4)
        load_wj(1)
        load_wj(2)
        load_wj(3)
        load_bias()
        load_wi(0,0,2)
        load_x(1,0,2)
        load_wi(0,2,4)
        load_x(1,2,4)
        load_wi(1,0,2)
        load_wi(1,2,4)
        nc.vector.memset(zeros[:], 0.0)
        warm(3,phi)
        tx(0,0)
        tx(0,1)
        twj(0,0,phi)
        tx(0,2)
        twj(0,1,phi)
        tx(0,3)
        twj(1,0,phi)
        tanh(0,0)
        tanh(0,1)
        tanh(0,2)
        tanh(0,3)
        cwj(0,0,vec)
        twj(1,1,phi)
        rnd2(0,0,0,1)
        rnd2(0,0,1,1)
        cwj(0,1,vec)
        rnd2(0,1,0,1)
        rnd2(0,1,1,1)
        twj(2,0,phi)
        twj(2,1,phi)
        rnd2(0,2,0,1)
        rnd2(0,2,1,1)
        qwj(0)
        cwj(1,0,sca)
        cwj(1,1,vec)
        rnd2(0,3,0,1)
        rnd2(0,3,1,1)
        qwj(1)
        qt(0)
        square(0,0)
        cwj(2,0,sca)
        cwj(2,1,sca)
        twj(3,0,front)
        twj(3,1,front)
        cwj(3,0,sca)
        cwj(3,1,sca)
        twi(0,0)
        om(0,0,"v")
        qwj(2)
        qwj(3)
        mm1(0,0)
        mm1(0,1)
        mm1(0,2)
        mm1(0,3)
        cwi(0,0,sca)
        square(0,1)
        tx(1,0)
        twi(0,1)
        tx(1,1)
        gatep(0,0)
        gatep(0,1)
        gatep(0,2)
        gatep(0,3)
        tanh(1,0)
        cwi(0,1,sca)
        mm1(0,4)
        mm1(0,5)
        twi(0,2)
        tx(1,2)
        mm1(0,6)
        mm1(0,7)
        twi(0,3)
        tanh(1,1)
        tx(1,3)
        cwi(0,2,sca)
        om(0,1,"v")
        regroup(0,0)
        gatep(0,4)
        qh(0,0)
        tanh(1,2)
        cwi(0,3,sca)
        tanh(1,3)
        twi(1,0)
        rnd2(1,0,0,2,"s")
        gatep(0,5)
        rnd2(1,0,1)
        gatep(0,6)
        gatep(0,7)
        cwi(1,0,sca)
        square(1,0)
        twi(1,1)
        twi(1,2)
        twi(1,3)
        qwi(0)
        regroup(0,1)
        rnd2(1,2,0)
        rnd2(1,2,1)
        qh(0,1)
        mm2(0,0,0,0,phi)
        mm2(0,1,0,0,phi)
        mm2(0,2,0,0,phi)
        mm2(0,3,0,0,phi)
        cwi(1,1,sca)
        cwi(1,2,sca)
        cwi(1,3,sca)
        square(1,1)
        mm2(0,0,0,1,phi)
        mm2(0,1,0,1,phi)
        mm2(0,2,0,1,phi)
        mm2(0,3,0,1,phi)
        qt(1)
        om(1,0,"v")
        qwi(1)
        mm1(1,0,front)
        mm1(1,1,front)
        mm1(1,2,front)
        mm1(1,3,front)
        store(0,0,0,sca)
        omp(1,4,6,"s")
        store(0,1,0,sca)
        store(0,2,0,sca)
        omp(1,6,8,"s")
        store(0,3,0,sca)
        gatep(1,0)
        gatep(1,1)
        gatep(1,2)
        gatep(1,3)
        mm1(1,4,front)
        mm1(1,5,front)
        mm1(1,6,front)
        mm1(1,7,front)
        mm2(0,0,1,0,phi)
        mm2(0,0,1,1,phi)
        mm2(0,1,1,0,phi)
        mm2(0,1,1,1,phi)
        mm2(0,2,1,0,phi)
        mm2(0,2,1,1,phi)
        mm2(0,3,1,0,phi)
        mm2(0,3,1,1,phi)
        store(0,0,1,sca)
        store(0,1,1,sca)
        store(0,2,1,sca)
        store(0,3,1,sca)
        gatep(1,4,0,256)
        regroup(1,0,0,256)
        gatep(1,5,0,256)
        gatep(1,6,0,256)
        gatep(1,7,0,256)
        qh(1,0,0,256)
        regroup(1,1,0,256)
        gatep(1,4,256,512)
        qh(1,1,0,256)
        regroup(1,0,256,512)
        gatep(1,5,256,512)
        gatep(1,6,256,512)
        gatep(1,7,256,512)
        qh(1,0,256,512)
        mm2(1,0,0,0,phi)
        mm2(1,0,0,1,phi)
        mm2(1,0,1,0,phi)
        mm2(1,0,1,1,phi)
        mm2(1,1,0,0,phi)
        mm2(1,1,0,1,phi)
        mm2(1,1,1,0,phi)
        mm2(1,1,1,1,phi)
        store(1,0,0,sca)
        store(1,0,1,sca)
        store(1,1,0,sca)
        store(1,1,1,sca)
        regroup(1,1,256,384)
        qh(1,1,256,384)
        regroup(1,1,384,512)
        qh(1,1,384,512)
        mm2(1,2,0,0,front)
        mm2(1,2,0,1,front)
        mm2(1,2,1,0,front)
        mm2(1,2,1,1,front)
        mm2(1,3,0,0,front)
        mm2(1,3,0,1,front)
        mm2(1,3,1,0,front)
        mm2(1,3,1,1,front)
        store(1,2,0,vec)
        store(1,2,1,sca)
        store(1,3,0,vec)
        store(1,3,1,sca)
